import numpy as np
import ml_dtypes


def mxq(x, axis, fmt="e4m3"):
    dtype, down = {"e4m3": (ml_dtypes.float8_e4m3fn, 7), "e5m2": (ml_dtypes.float8_e5m2, 14)}[fmt]
    v = np.moveaxis(np.asarray(x, np.float32).astype(ml_dtypes.bfloat16).astype(np.float64), axis, -1)
    blocks = v.reshape(v.shape[:-1] + (-1, 32))
    amax = np.abs(blocks).max(-1, keepdims=True)
    byte = np.maximum(np.where(amax > 0, np.frexp(amax)[1] - 1 + 127, 0) - down, 1)
    scale = np.exp2(byte - 127.0)
    codes = (blocks / scale).astype(np.float32).astype(dtype).astype(np.float64)
    return np.moveaxis((codes * scale).reshape(v.shape), -1, axis)


WIDE = False


def mx_kscale(k):
    if not WIDE:
        return np.ones(k)
    levels = np.array([10, -10, 5, -5, 0])
    a = np.random.permutation(np.resize(levels, k // 512 * 4)).reshape(k // 512, 4)
    idx = np.arange(k)
    return np.exp2(a[idx // 512, idx % 128 // 32])


BF16 = ml_dtypes.bfloat16


def bf(x):
    return np.asarray(x, np.float32).astype(BF16)


def f64(x):
    return np.asarray(x).astype(np.float64)


NQ, NK, D, DV = 2048, 2048, 256, 256
EPS = 1e-7
L = D // 32


def ball_points(n, p, kap):
    d = np.random.standard_normal((n, L)) @ p + 0.5 * np.random.standard_normal((n, D)) / np.sqrt(D)
    d = d / np.linalg.norm(d, axis=-1, keepdims=True)
    return d * (0.5 + 0.4 * np.random.random((n, 1))) / np.sqrt(kap)


def setup_inputs():
    c = bf(-(0.05 + 0.02 * np.random.random(1)))
    kap = np.abs(f64(c))[0]
    p = np.random.standard_normal((L, D)) / np.sqrt(D)
    t = mx_kscale(NK)
    t = t / t.max()
    q = ball_points(NQ, p, kap) * (0.5 + 0.5 * t.min())
    k = ball_points(NK, p, kap)
    r = np.sqrt(kap) * np.linalg.norm(k, axis=-1)
    a = (1.0 - r) / (1.0 + r) * t ** np.sqrt(kap)
    k = k * ((1.0 - a) / (1.0 + a) / r)[:, None]
    v = np.random.standard_normal((NK, DV)) * 2.0 * t.mean() / t[:, None]
    return {"query": bf(q), "keys": bf(k), "values": bf(v), "c": c}


def reference(query, keys, values, c):
    query, keys, values, c = f64(query), f64(keys), f64(values), f64(c)
    c_cl = np.clip(np.abs(c) + EPS, EPS, 1.0 - EPS)
    c_sqrt = np.sqrt(c_cl)

    uu = np.sum(query * query, axis=-1)
    vv = np.sum(keys * keys, axis=-1)
    uu_c = np.minimum(c_cl * uu, 1.0 - EPS)
    vv_c = np.minimum(c_cl * vv, 1.0 - EPS)

    diff_sq = np.maximum(uu[:, None] + vv[None, :] - 2.0 * (query @ keys.T), 0.0)

    denom = np.maximum((1.0 - uu_c)[:, None] * (1.0 - vv_c)[None, :], EPS)
    arg = np.maximum(1.0 + 2.0 * c_cl * diff_sq / denom, 1.0 + EPS)
    dist = np.arccosh(arg) / c_sqrt
    dist = np.nan_to_num(dist, nan=100.0, posinf=100.0, neginf=-100.0)

    z = -dist
    e = np.exp(z - z.max(-1, keepdims=True))
    weights = e / e.sum(-1, keepdims=True)
    weights = np.nan_to_num(weights, nan=0.0)
    return mxq(weights, 1, "e4m3") @ mxq(values, 0, "e4m3")

@@ -1,0 +1,350 @@
+from contextlib import ExitStack
+
+import concourse.mybir as mybir
+from concourse.masks import make_identity
+
+F32 = mybir.dt.float32
+BF16 = mybir.dt.bfloat16
+U32 = mybir.dt.uint32
+U8 = mybir.dt.uint8
+FP8X4 = mybir.dt.float8_e4m3fn_x4
+ALU = mybir.AluOpType
+ACT = mybir.ActivationFunctionType
+
+NQ, NK, D, DV = 2048, 2048, 256, 256
+EPS = 1e-7
+P = 128
+Q_TILES = NQ // P
+K_TILES = NK // P
+D_HALVES = D // P
+BANK = 512
+BANKS_PER_ROW = NK // BANK
+TURNS = BANK // P
+PACK = 4
+K_PASS = P * PACK
+PASSES = NK // K_PASS
+GROUP = 4
+N_GROUPS = Q_TILES // GROUP
+
+FLOPS = 2 * NQ * NK * D + 2 * NQ * NK * DV
+
+
+def tile_hyperbolicattention_kernel(tc, query, keys, values, c, out):
+    nc = tc.nc
+    with ExitStack() as ctx:
+        ctx.enter_context(tc.manual_schedule())
+        keep = ctx.enter_context(tc.tile_pool(name="keep", bufs=1))
+        setup = ctx.enter_context(tc.tile_pool(name="setup", bufs=1))
+        rows = ctx.enter_context(tc.tile_pool(name="rows", bufs=2 * GROUP))
+        roots = ctx.enter_context(tc.tile_pool(name="roots", bufs=GROUP))
+        tail = ctx.enter_context(tc.tile_pool(name="tail", bufs=2))
+        psum_scores = ctx.enter_context(tc.psum_pool(name="psum_scores", bufs=BANKS_PER_ROW))
+        psum_turn = ctx.enter_context(tc.psum_pool(name="psum_turn", bufs=2))
+        psum_out = ctx.enter_context(tc.psum_pool(name="psum_out", bufs=2))
+
+        c_bf = keep.tile([P, 1], BF16, name="c_bf")
+        nc.sync.dma_start(out=c_bf[:], in_=c.partition_broadcast(P))
+        k_nat = setup.tile([P, K_TILES, D], BF16, name="k_nat")
+        q_nat = setup.tile([P, Q_TILES, D], BF16, name="q_nat")
+        for nat, dram in ((k_nat, keys), (q_nat, query)):
+            view = dram.rearrange("(t p) d -> p t d", p=P)
+            for t0 in range(0, K_TILES, TURNS):
+                nc.sync.dma_start(out=nat[:, t0 : t0 + TURNS, :], in_=view[:, t0 : t0 + TURNS, :])
+        v_raw = setup.tile([P, PASSES, PACK, DV], BF16, name="v_raw")
+        nc.sync.dma_start(
+            out=v_raw[:], in_=values.rearrange("(g p j) w -> p g j w", g=PASSES, p=P, j=PACK)
+        )
+
+        ident_bf = keep.tile([P, P], BF16, name="ident_bf")
+        make_identity(nc, ident_bf[:])
+        ident_f32 = keep.tile([P, P], F32, name="ident_f32")
+        make_identity(nc, ident_f32[:])
+
+        one = keep.tile([P, 1], F32, name="one")
+        nc.vector.memset(one[:], 1.0)
+        warm = keep.tile([P, 1], F32, name="warm")
+        nc.scalar.activation(out=warm[:], in_=one[:], func=ACT.Sqrt)
+
+        kappa = keep.tile([P, 1], F32, name="kappa")
+        nc.scalar.activation(out=kappa[:], in_=c_bf[:], func=ACT.Abs)
+        nc.vector.tensor_scalar(
+            out=kappa[:], in0=kappa[:], scalar1=EPS, scalar2=EPS, op0=ALU.add, op1=ALU.max
+        )
+        nc.vector.tensor_scalar(
+            out=kappa[:], in0=kappa[:], scalar1=1.0 - EPS, scalar2=None, op0=ALU.min
+        )
+        neg_p = keep.tile([P, 1], F32, name="neg_p")
+        nc.scalar.activation(out=neg_p[:], in_=kappa[:], func=ACT.Sqrt)
+        nc.vector.reciprocal(out=neg_p[:], in_=neg_p[:])
+        nc.vector.tensor_scalar(
+            out=neg_p[:], in0=neg_p[:], scalar1=-2.0, scalar2=None, op0=ALU.mult
+        )
+
+        squares = setup.tile([P, K_TILES + Q_TILES, D], BF16, name="squares")
+        vv = setup.tile([P, K_TILES], F32, name="vv")
+        uu = setup.tile([P, Q_TILES], F32, name="uu")
+        kT = keep.tile([P, D_HALVES, NK], BF16, name="kT")
+        qT = keep.tile([P, D_HALVES, NQ], BF16, name="qT")
+
+        def turn_features(nat, t0, copy, dst):
+            for h in range(D_HALVES):
+                turned = psum_scores.tile([P, TURNS, P], BF16, name="turned_bf", tag="scores")
+                for r in range(TURNS):
+                    nc.tensor.transpose(
+                        turned[:, r, :], nat[:, t0 + r, h * P : (h + 1) * P], ident_bf[:]
+                    )
+                copy(
+                    out=dst[:, h, t0 * P : (t0 + TURNS) * P],
+                    in_=turned[:].rearrange("p r m -> p (r m)"),
+                )
+
+        for t0 in range(0, K_TILES, TURNS):
+            for t in range(t0, t0 + TURNS):
+                nc.scalar.activation(
+                    out=squares[:, t, :], in_=k_nat[:, t, :], func=ACT.Square,
+                    accum_out=vv[:, t : t + 1],
+                )
+            turn_features(k_nat, t0, nc.vector.tensor_copy, kT)
+        for t0 in range(0, Q_TILES, TURNS):
+            turn_features(q_nat, t0, nc.scalar.copy, qT)
+
+        def one_minus_clipped(dst, sq_norms):
+            nc.vector.tensor_scalar(
+                out=dst, in0=sq_norms, scalar1=kappa[:, 0:1], scalar2=1.0 - EPS,
+                op0=ALU.mult, op1=ALU.min,
+            )
+            nc.vector.tensor_scalar(
+                out=dst, in0=dst, scalar1=-1.0, scalar2=1.0, op0=ALU.mult, op1=ALU.add
+            )
+
+        kb_neg = setup.tile([P, K_TILES], F32, name="kb_neg")
+        one_minus_clipped(kb_neg[:], vv[:])
+        nc.vector.reciprocal(out=kb_neg[:], in_=kb_neg[:])
+        nc.vector.tensor_scalar(
+            out=kb_neg[:], in0=kb_neg[:], scalar1=kappa[:, 0:1], scalar2=-2.0,
+            op0=ALU.mult, op1=ALU.mult,
+        )
+        vv_half = setup.tile([P, K_TILES], F32, name="vv_half")
+        nc.vector.tensor_scalar(
+            out=vv_half[:], in0=vv[:], scalar1=0.5, scalar2=None, op0=ALU.mult
+        )
+
+        vv_half_row = keep.tile([P, NK], F32, name="vv_half_row")
+        kb_neg_row = keep.tile([P, NK], F32, name="kb_neg_row")
+        repeated = []
+        for name, per_key in (("rep_vv", vv_half), ("rep_kb", kb_neg)):
+            rep = setup.tile([P, K_TILES, P], F32, name=name)
+            nc.vector.tensor_copy(
+                out=rep[:], in_=per_key[:].unsqueeze(2).to_broadcast([P, K_TILES, P])
+            )
+            repeated.append(rep)
+        for rep, row in zip(repeated, (vv_half_row, kb_neg_row)):
+            for t0 in range(0, K_TILES, TURNS):
+                turned = psum_turn.tile([P, TURNS, P], F32, name="turned_rep", tag="turn")
+                for r in range(TURNS):
+                    nc.tensor.transpose(turned[:, r, :], rep[:, t0 + r, :], ident_f32[:])
+                nc.vector.tensor_copy(
+                    out=row[:, t0 * P : (t0 + TURNS) * P],
+                    in_=turned[:].rearrange("p r m -> p (r m)"),
+                )
+
+        for t in range(Q_TILES):
+            nc.scalar.activation(
+                out=squares[:, K_TILES + t, :], in_=q_nat[:, t, :], func=ACT.Square,
+                accum_out=uu[:, t : t + 1],
+            )
+        a_q = keep.tile([P, Q_TILES], F32, name="a_q")
+        one_minus_clipped(a_q[:], uu[:])
+        uu_half = keep.tile([P, Q_TILES], F32, name="uu_half")
+        nc.vector.tensor_scalar(
+            out=uu_half[:], in0=uu[:], scalar1=0.5, scalar2=None, op0=ALU.mult
+        )
+        m_neg = keep.tile([P, Q_TILES], F32, name="m_neg")
+        nc.vector.tensor_scalar(
+            out=m_neg[:], in0=a_q[:], scalar1=kappa[:, 0:1], scalar2=-2.0 / EPS,
+            op0=ALU.mult, op1=ALU.mult,
+        )
+        h_floor = keep.tile([P, Q_TILES], F32, name="h_floor")
+        nc.vector.tensor_scalar(
+            out=h_floor[:], in0=a_q[:], scalar1=EPS / 2.0, scalar2=None, op0=ALU.mult
+        )
+
+        v_grouped = setup.tile([P, PASSES, DV, PACK], BF16, name="v_grouped", align_bytes=64)
+        nc.scalar.copy(out=v_grouped[:], in_=v_raw[:].rearrange("p g j w -> p g w j"))
+        v_codes = keep.tile([P, PASSES * DV], U32, name="v_codes", align_bytes=64)
+        v_scales = keep.tile([P, PASSES * DV], U8, name="v_scales", align_bytes=64)
+
+        h_pair = keep.tile([P, 2, Q_TILES], F32, name="h_pair")
+        r_pair = keep.tile([P, 2, Q_TILES], F32, name="r_pair")
+        inv_s_min = keep.tile([P, Q_TILES], F32, name="inv_s_min")
+        e_sum = keep.tile([P, Q_TILES], F32, name="e_sum")
+        r_sum = keep.tile([P, Q_TILES], F32, name="r_sum")
+
+        score_bank = {}
+        row_of = {}
+        root_of = {}
+        weights_of = {}
+        turned_of = {}
+        grouped_of = {}
+        product_of = {}
+
+        def scores(i, bank):
+            ps = psum_scores.tile([P, BANK], F32, name="ps", tag="scores")
+            for h in range(D_HALVES):
+                nc.tensor.matmul(
+                    ps[:],
+                    lhsT=qT[:, h, i * P : (i + 1) * P],
+                    rhs=kT[:, h, bank * BANK : (bank + 1) * BANK],
+                    start=(h == 0),
+                    stop=(h == D_HALVES - 1),
+                )
+            score_bank[(i, bank)] = ps
+
+        def distance_term(i):
+            row = rows.tile([P, NK], F32, name="row", tag="row")
+            row_of[i] = row
+            for bank in range(BANKS_PER_ROW):
+                cols = slice(bank * BANK, (bank + 1) * BANK)
+                nc.vector.scalar_tensor_tensor(
+                    out=row[:, cols], in0=score_bank[(i, bank)][:], scalar=uu_half[:, i : i + 1],
+                    in1=vv_half_row[:, cols], op0=ALU.subtract, op1=ALU.subtract,
+                )
+                if i + 1 < Q_TILES:
+                    scores(i + 1, bank)
+            nc.vector.scalar_tensor_tensor(
+                out=row[:], in0=kb_neg_row[:], scalar=m_neg[:, i : i + 1], in1=row[:],
+                op0=ALU.max, op1=ALU.mult,
+            )
+            nc.vector.tensor_scalar(
+                out=row[:], in0=row[:], scalar1=h_floor[:, i : i + 1], scalar2=None,
+                op0=ALU.max, op1=ALU.min, accum_out=h_pair[:, 0, i : i + 1],
+            )
+
+        def square_roots(i):
+            root = roots.tile([P, NK], F32, name="root", tag="root")
+            root_of[i] = root
+            nc.scalar.activation(out=root[:], in_=row_of[i][:], func=ACT.Sqrt)
+            nc.scalar.activation(
+                out=row_of[i][:], in_=row_of[i][:], func=ACT.Sqrt, bias=a_q[:, i : i + 1]
+            )
+
+        def normalise(i):
+            weights = tail.tile([P, NK], BF16, name="weights", tag="weights")
+            weights_of[i] = weights
+            nc.vector.tensor_scalar(
+                out=weights[:], in0=row_of[i][:], scalar1=r_sum[:, i : i + 1], scalar2=None,
+                op0=ALU.mult,
+            )
+
+        def turn_weights(i):
+            words = weights_of[i][:].bitcast(F32).rearrange(
+                "p (g m u) -> p g u m", g=PASSES, m=P, u=2
+            )
+            turned_of[i] = []
+            for half in range(2):
+                turned = psum_turn.tile([P, 2, 2, P], F32, name="turned_w", tag="turn")
+                for g in range(2):
+                    for u in range(2):
+                        nc.tensor.transpose(
+                            turned[:, g, u, :], words[:, 2 * half + g, u, :], ident_f32[:]
+                        )
+                turned_of[i].append(turned)
+
+        def group_weights(i):
+            grouped = tail.tile([P, NK], BF16, name="grouped", tag="grouped", align_bytes=64)
+            grouped_of[i] = grouped
+            words = grouped[:].bitcast(F32).rearrange("p (g q u) -> p g q u", g=PASSES, q=P, u=2)
+            for half in range(2):
+                nc.vector.tensor_copy(
+                    out=words[:, 2 * half : 2 * half + 2, :, :],
+                    in_=turned_of[i][half][:].rearrange("p g u q -> p g q u"),
+                )
+
+        def quantise_and_multiply(i):
+            codes = tail.tile([P, PASSES * P], U32, name="codes", tag="codes", align_bytes=64)
+            scales = tail.tile([P, PASSES * P], U8, name="scales", tag="scales", align_bytes=64)
+            nc.vector.quantize_mx(
+                out=codes[:].bitcast(FP8X4), scales=scales[:], in_=grouped_of[i][:]
+            )
+            product = psum_out.tile([P, DV], F32, name="product", tag="product")
+            product_of[i] = product
+            for g in range(PASSES):
+                nc.tensor.matmul_mx(
+                    out=product[:],
+                    lhsT=codes[:, g * P : (g + 1) * P].bitcast(FP8X4),
+                    lhsT_scale=scales[:, g * P : (g + 1) * P],
+                    rhs=v_codes[:, g * DV : (g + 1) * DV].bitcast(FP8X4),
+                    rhs_scale=v_scales[:, g * DV : (g + 1) * DV],
+                    start=(g == 0),
+                    stop=(g == PASSES - 1),
+                )
+
+        def store(i):
+            result = tail.tile([P, DV], F32, name="result", tag="result", bufs=GROUP)
+            nc.scalar.copy(out=result[:], in_=product_of[i][:])
+            nc.sync.dma_start(out=out[i * P : (i + 1) * P, :], in_=result[:])
+
+        def tiles_of(g):
+            return list(range(g * GROUP, (g + 1) * GROUP)) if 0 <= g < N_GROUPS else []
+
+        def distance_terms(group):
+            for i in group:
+                distance_term(i)
+            if group:
+                cols = slice(group[0], group[-1] + 1)
+                nc.vector.tensor_add(
+                    out=h_pair[:, 1, cols], in0=h_pair[:, 0, cols], in1=a_q[:, cols]
+                )
+
+        for bank in range(BANKS_PER_ROW):
+            scores(0, bank)
+        distance_terms(tiles_of(0))
+        nc.vector.quantize_mx(
+            out=v_codes[:].bitcast(FP8X4),
+            scales=v_scales[:],
+            in_=v_grouped[:].rearrange("p g w j -> p (g w j)"),
+        )
+
+        for g in range(N_GROUPS + 1):
+            cur, old, nxt = tiles_of(g), tiles_of(g - 1), tiles_of(g + 1)
+
+            for i in cur:
+                square_roots(i)
+            if cur:
+                cols = slice(cur[0], cur[-1] + 1)
+                nc.scalar.activation(out=r_pair[:, :, cols], in_=h_pair[:, :, cols], func=ACT.Sqrt)
+
+            if old:
+                cols = slice(old[0], old[-1] + 1)
+                nc.vector.reciprocal(out=r_sum[:, cols], in_=e_sum[:, cols])
+            for step in range(len(old) + 3):
+                if step < len(old):
+                    normalise(old[step])
+                if 0 <= step - 1 < len(old):
+                    group_weights(old[step - 1])
+                if step < len(old):
+                    turn_weights(old[step])
+                if 0 <= step - 2 < len(old):
+                    quantise_and_multiply(old[step - 2])
+                if 0 <= step - 3 < len(old):
+                    store(old[step - 3])
+
+            for i in cur:
+                if i == cur[-1]:
+                    cols = slice(cur[0], cur[-1] + 1)
+                    nc.vector.tensor_add(
+                        out=inv_s_min[:, cols], in0=r_pair[:, 0, cols], in1=r_pair[:, 1, cols]
+                    )
+                    nc.vector.reciprocal(out=inv_s_min[:, cols], in_=inv_s_min[:, cols])
+                nc.vector.tensor_add(out=row_of[i][:], in0=row_of[i][:], in1=root_of[i][:])
+
+            for i in cur:
+                nc.scalar.activation(
+                    out=row_of[i][:], in_=row_of[i][:], func=ACT.Ln, scale=inv_s_min[:, i : i + 1]
+                )
+            distance_terms(nxt)
+            for i in cur:
+                nc.scalar.activation(
+                    out=row_of[i][:], in_=row_of[i][:], func=ACT.Exp, scale=neg_p[:, 0:1],
+                    accum_out=e_sum[:, i : i + 1],
+                )

@@ -25,6 +25,7 @@ K_PASS = P * PACK
 PASSES = NK // K_PASS
 GROUP = 4
 N_GROUPS = Q_TILES // GROUP
+AHEAD = 2
 
 FLOPS = 2 * NQ * NK * D + 2 * NQ * NK * DV
 
@@ -229,11 +230,12 @@ def tile_hyperbolicattention_kernel(tc, query, keys, values, c, out):
             )
 
         def normalise(i):
-            weights = tail.tile([P, NK], BF16, name="weights", tag="weights")
+            nc.vector.reciprocal(out=r_sum[:, i : i + 1], in_=e_sum[:, i : i + 1])
+            weights = tail.tile([P, NK], BF16, name="weights", tag="weights", bufs=GROUP)
             weights_of[i] = weights
-            nc.vector.tensor_scalar(
-                out=weights[:], in0=row_of[i][:], scalar1=r_sum[:, i : i + 1], scalar2=None,
-                op0=ALU.mult,
+            nc.gpsimd.tensor_scalar(
+                out=weights[:], in0=row_of[i][:], scalar1=r_sum[:, i : i + 1], scalar2=0.0,
+                op0=ALU.mult, op1=ALU.add,
             )
 
         def turn_weights(i):
@@ -266,11 +268,13 @@ def tile_hyperbolicattention_kernel(tc, query, keys, values, c, out):
             nc.vector.quantize_mx(
                 out=codes[:].bitcast(FP8X4), scales=scales[:], in_=grouped_of[i][:]
             )
-            product = psum_out.tile([P, DV], F32, name="product", tag="product")
-            product_of[i] = product
+            if i % 2 == 0:
+                pair = psum_out.tile([P, 2, DV], F32, name="pair", tag="pair")
+                product_of[i] = pair[:, 0, :]
+                product_of[i + 1] = pair[:, 1, :]
             for g in range(PASSES):
                 nc.tensor.matmul_mx(
-                    out=product[:],
+                    out=product_of[i],
                     lhsT=codes[:, g * P : (g + 1) * P].bitcast(FP8X4),
                     lhsT_scale=scales[:, g * P : (g + 1) * P],
                     rhs=v_codes[:, g * DV : (g + 1) * DV].bitcast(FP8X4),
@@ -281,7 +285,7 @@ def tile_hyperbolicattention_kernel(tc, query, keys, values, c, out):
 
         def store(i):
             result = tail.tile([P, DV], F32, name="result", tag="result", bufs=GROUP)
-            nc.scalar.copy(out=result[:], in_=product_of[i][:])
+            nc.scalar.copy(out=result[:], in_=product_of[i])
             nc.sync.dma_start(out=out[i * P : (i + 1) * P, :], in_=result[:])
 
         def tiles_of(g):
@@ -314,34 +318,36 @@ def tile_hyperbolicattention_kernel(tc, query, keys, values, c, out):
                 cols = slice(cur[0], cur[-1] + 1)
                 nc.scalar.activation(out=r_pair[:, :, cols], in_=h_pair[:, :, cols], func=ACT.Sqrt)
 
-            if old:
-                cols = slice(old[0], old[-1] + 1)
-                nc.vector.reciprocal(out=r_sum[:, cols], in_=e_sum[:, cols])
-            for step in range(len(old) + 3):
-                if step < len(old):
-                    normalise(old[step])
-                if 0 <= step - 1 < len(old):
-                    group_weights(old[step - 1])
-                if step < len(old):
-                    turn_weights(old[step])
-                if 0 <= step - 2 < len(old):
-                    quantise_and_multiply(old[step - 2])
-                if 0 <= step - 3 < len(old):
-                    store(old[step - 3])
-
-            for i in cur:
-                if i == cur[-1]:
-                    cols = slice(cur[0], cur[-1] + 1)
-                    nc.vector.tensor_add(
-                        out=inv_s_min[:, cols], in0=r_pair[:, 0, cols], in1=r_pair[:, 1, cols]
-                    )
-                    nc.vector.reciprocal(out=inv_s_min[:, cols], in_=inv_s_min[:, cols])
-                nc.vector.tensor_add(out=row_of[i][:], in0=row_of[i][:], in1=root_of[i][:])
+            for i in old[:AHEAD]:
+                normalise(i)
+            for j in range(GROUP + 1):
+                if j + AHEAD < len(old):
+                    normalise(old[j + AHEAD])
+                if j < len(old):
+                    turn_weights(old[j])
+                if j < len(cur):
+                    i = cur[j]
+                    if i == cur[-1]:
+                        cols = slice(cur[0], cur[-1] + 1)
+                        nc.vector.tensor_add(
+                            out=inv_s_min[:, cols], in0=r_pair[:, 0, cols], in1=r_pair[:, 1, cols]
+                        )
+                        nc.vector.reciprocal(out=inv_s_min[:, cols], in_=inv_s_min[:, cols])
+                    nc.vector.tensor_add(out=row_of[i][:], in0=row_of[i][:], in1=root_of[i][:])
+                if j < len(old):
+                    group_weights(old[j])
+                if 0 <= j - 1 < len(old):
+                    quantise_and_multiply(old[j - 1])
+                    if not cur:
+                        store(old[j - 1])
 
             for i in cur:
                 nc.scalar.activation(
                     out=row_of[i][:], in_=row_of[i][:], func=ACT.Ln, scale=inv_s_min[:, i : i + 1]
                 )
+            if cur:
+                for i in old:
+                    store(i)
             distance_terms(nxt)
             for i in cur:
                 nc.scalar.activation(

@@ -25,7 +25,11 @@ K_PASS = P * PACK
 PASSES = NK // K_PASS
 GROUP = 4
 N_GROUPS = Q_TILES // GROUP
+JUNK_SLOTS = 8
 AHEAD = 2
+
+assert GROUP == TURNS
+assert D_HALVES == 2
 
 FLOPS = 2 * NQ * NK * D + 2 * NQ * NK * DV
 
@@ -81,15 +85,22 @@ def tile_hyperbolicattention_kernel(tc, query, keys, values, c, out):
             out=neg_p[:], in0=neg_p[:], scalar1=-2.0, scalar2=None, op0=ALU.mult
         )
 
-        squares = setup.tile([P, K_TILES + Q_TILES, D], BF16, name="squares")
+        squares = setup.tile([P, JUNK_SLOTS, D], BF16, name="squares")
         vv = setup.tile([P, K_TILES], F32, name="vv")
         uu = setup.tile([P, Q_TILES], F32, name="uu")
         kT = keep.tile([P, D_HALVES, NK], BF16, name="kT")
         qT = keep.tile([P, D_HALVES, NQ], BF16, name="qT")
 
-        def turn_features(nat, t0, copy, dst):
+        def squared_norms(nat, t0, sums):
+            for t in range(t0, t0 + TURNS):
+                nc.scalar.activation(
+                    out=squares[:, t % JUNK_SLOTS, :], in_=nat[:, t, :], func=ACT.Square,
+                    accum_out=sums[:, t : t + 1],
+                )
+
+        def turn_features(nat, t0, pool, tag, copy, dst):
             for h in range(D_HALVES):
-                turned = psum_scores.tile([P, TURNS, P], BF16, name="turned_bf", tag="scores")
+                turned = pool.tile([P, TURNS, P], BF16, name="turned_bf", tag=tag)
                 for r in range(TURNS):
                     nc.tensor.transpose(
                         turned[:, r, :], nat[:, t0 + r, h * P : (h + 1) * P], ident_bf[:]
@@ -100,14 +111,12 @@ def tile_hyperbolicattention_kernel(tc, query, keys, values, c, out):
                 )
 
         for t0 in range(0, K_TILES, TURNS):
-            for t in range(t0, t0 + TURNS):
-                nc.scalar.activation(
-                    out=squares[:, t, :], in_=k_nat[:, t, :], func=ACT.Square,
-                    accum_out=vv[:, t : t + 1],
-                )
-            turn_features(k_nat, t0, nc.vector.tensor_copy, kT)
+            squared_norms(k_nat, t0, vv)
+            turn_features(k_nat, t0, psum_scores, "scores", nc.vector.tensor_copy, kT)
         for t0 in range(0, Q_TILES, TURNS):
-            turn_features(q_nat, t0, nc.scalar.copy, qT)
+            squared_norms(q_nat, t0, uu)
+        v_grouped = setup.tile([P, PASSES, DV, PACK], BF16, name="v_grouped", align_bytes=64)
+        nc.scalar.copy(out=v_grouped[:], in_=v_raw[:].rearrange("p g j w -> p g w j"))
 
         def one_minus_clipped(dst, sq_norms):
             nc.vector.tensor_scalar(
@@ -118,6 +127,37 @@ def tile_hyperbolicattention_kernel(tc, query, keys, values, c, out):
                 out=dst, in0=dst, scalar1=-1.0, scalar2=1.0, op0=ALU.mult, op1=ALU.add
             )
 
+        def repeat(rep, per_row):
+            nc.vector.tensor_copy(out=rep, in_=per_row.unsqueeze(2).to_broadcast(rep.shape))
+
+        def spread(row, rep):
+            turned = psum_turn.tile([P, TURNS, P], F32, name="turned_rep", tag="turn")
+            for r in range(TURNS):
+                nc.tensor.transpose(turned[:, r, :], rep[:, r, :], ident_f32[:])
+            nc.vector.tensor_copy(out=row, in_=turned[:].rearrange("p r m -> p (r m)"))
+
+        vv_term = setup.tile([P, K_TILES], F32, name="vv_term")
+        nc.vector.tensor_scalar(
+            out=vv_term[:], in0=vv[:], scalar1=-0.5, scalar2=None, op0=ALU.mult
+        )
+        rep_vv = keep.tile([P, K_TILES, P], F32, name="rep_vv")
+        repeat(rep_vv[:], vv_term[:])
+
+        uu_term = setup.tile([P, Q_TILES], F32, name="uu_term")
+        uu_row = keep.tile([P, NQ], F32, name="uu_row")
+
+        def prepare_queries(t0):
+            turn_features(q_nat, t0, psum_turn, "turn", nc.vector.tensor_copy, qT)
+            block = slice(t0, t0 + TURNS)
+            nc.vector.tensor_scalar(
+                out=uu_term[:, block], in0=uu[:, block], scalar1=-0.5, scalar2=None, op0=ALU.mult
+            )
+            rep_uu = tail.tile([P, TURNS, P], F32, name="rep_uu", tag="rep_uu")
+            repeat(rep_uu[:], uu_term[:, block])
+            spread(uu_row[:, t0 * P : (t0 + TURNS) * P], rep_uu)
+
+        prepare_queries(0)
+
         kb_neg = setup.tile([P, K_TILES], F32, name="kb_neg")
         one_minus_clipped(kb_neg[:], vv[:])
         nc.vector.reciprocal(out=kb_neg[:], in_=kb_neg[:])
@@ -125,41 +165,14 @@ def tile_hyperbolicattention_kernel(tc, query, keys, values, c, out):
             out=kb_neg[:], in0=kb_neg[:], scalar1=kappa[:, 0:1], scalar2=-2.0,
             op0=ALU.mult, op1=ALU.mult,
         )
-        vv_half = setup.tile([P, K_TILES], F32, name="vv_half")
-        nc.vector.tensor_scalar(
-            out=vv_half[:], in0=vv[:], scalar1=0.5, scalar2=None, op0=ALU.mult
-        )
-
-        vv_half_row = keep.tile([P, NK], F32, name="vv_half_row")
+        rep_kb = setup.tile([P, K_TILES, P], F32, name="rep_kb")
+        repeat(rep_kb[:], kb_neg[:])
         kb_neg_row = keep.tile([P, NK], F32, name="kb_neg_row")
-        repeated = []
-        for name, per_key in (("rep_vv", vv_half), ("rep_kb", kb_neg)):
-            rep = setup.tile([P, K_TILES, P], F32, name=name)
-            nc.vector.tensor_copy(
-                out=rep[:], in_=per_key[:].unsqueeze(2).to_broadcast([P, K_TILES, P])
-            )
-            repeated.append(rep)
-        for rep, row in zip(repeated, (vv_half_row, kb_neg_row)):
-            for t0 in range(0, K_TILES, TURNS):
-                turned = psum_turn.tile([P, TURNS, P], F32, name="turned_rep", tag="turn")
-                for r in range(TURNS):
-                    nc.tensor.transpose(turned[:, r, :], rep[:, t0 + r, :], ident_f32[:])
-                nc.vector.tensor_copy(
-                    out=row[:, t0 * P : (t0 + TURNS) * P],
-                    in_=turned[:].rearrange("p r m -> p (r m)"),
-                )
+        for t0 in range(0, K_TILES, TURNS):
+            spread(kb_neg_row[:, t0 * P : (t0 + TURNS) * P], rep_kb[:, t0 : t0 + TURNS, :])
 
-        for t in range(Q_TILES):
-            nc.scalar.activation(
-                out=squares[:, K_TILES + t, :], in_=q_nat[:, t, :], func=ACT.Square,
-                accum_out=uu[:, t : t + 1],
-            )
         a_q = keep.tile([P, Q_TILES], F32, name="a_q")
         one_minus_clipped(a_q[:], uu[:])
-        uu_half = keep.tile([P, Q_TILES], F32, name="uu_half")
-        nc.vector.tensor_scalar(
-            out=uu_half[:], in0=uu[:], scalar1=0.5, scalar2=None, op0=ALU.mult
-        )
         m_neg = keep.tile([P, Q_TILES], F32, name="m_neg")
         nc.vector.tensor_scalar(
             out=m_neg[:], in0=a_q[:], scalar1=kappa[:, 0:1], scalar2=-2.0 / EPS,
@@ -169,11 +182,6 @@ def tile_hyperbolicattention_kernel(tc, query, keys, values, c, out):
         nc.vector.tensor_scalar(
             out=h_floor[:], in0=a_q[:], scalar1=EPS / 2.0, scalar2=None, op0=ALU.mult
         )
-
-        v_grouped = setup.tile([P, PASSES, DV, PACK], BF16, name="v_grouped", align_bytes=64)
-        nc.scalar.copy(out=v_grouped[:], in_=v_raw[:].rearrange("p g j w -> p g w j"))
-        v_codes = keep.tile([P, PASSES * DV], U32, name="v_codes", align_bytes=64)
-        v_scales = keep.tile([P, PASSES * DV], U8, name="v_scales", align_bytes=64)
 
         h_pair = keep.tile([P, 2, Q_TILES], F32, name="h_pair")
         r_pair = keep.tile([P, 2, Q_TILES], F32, name="r_pair")
@@ -191,33 +199,37 @@ def tile_hyperbolicattention_kernel(tc, query, keys, values, c, out):
 
         def scores(i, bank):
             ps = psum_scores.tile([P, BANK], F32, name="ps", tag="scores")
-            for h in range(D_HALVES):
-                nc.tensor.matmul(
-                    ps[:],
-                    lhsT=qT[:, h, i * P : (i + 1) * P],
-                    rhs=kT[:, h, bank * BANK : (bank + 1) * BANK],
-                    start=(h == 0),
-                    stop=(h == D_HALVES - 1),
-                )
+            queries = slice(i * P, (i + 1) * P)
+            keys_of_bank = slice(bank * BANK, (bank + 1) * BANK)
+            nc.tensor.matmul(
+                ps[:], lhsT=qT[:, 0, queries], rhs=kT[:, 0, keys_of_bank], start=True, stop=False
+            )
+            for r in range(TURNS):
+                for term in (rep_vv[:, bank * TURNS + r, :], uu_row[:, queries]):
+                    nc.tensor.matmul(
+                        ps[:, r * P : (r + 1) * P], lhsT=term, rhs=ident_f32[:],
+                        is_transpose=True, start=False, stop=False,
+                    )
+            nc.tensor.matmul(
+                ps[:], lhsT=qT[:, 1, queries], rhs=kT[:, 1, keys_of_bank], start=False, stop=True
+            )
             score_bank[(i, bank)] = ps
 
-        def distance_term(i):
+        def scaled_differences(i):
             row = rows.tile([P, NK], F32, name="row", tag="row")
             row_of[i] = row
             for bank in range(BANKS_PER_ROW):
                 cols = slice(bank * BANK, (bank + 1) * BANK)
                 nc.vector.scalar_tensor_tensor(
-                    out=row[:, cols], in0=score_bank[(i, bank)][:], scalar=uu_half[:, i : i + 1],
-                    in1=vv_half_row[:, cols], op0=ALU.subtract, op1=ALU.subtract,
+                    out=row[:, cols], in0=kb_neg_row[:, cols], scalar=m_neg[:, i : i + 1],
+                    in1=score_bank[(i, bank)][:], op0=ALU.max, op1=ALU.mult,
                 )
                 if i + 1 < Q_TILES:
                     scores(i + 1, bank)
-            nc.vector.scalar_tensor_tensor(
-                out=row[:], in0=kb_neg_row[:], scalar=m_neg[:, i : i + 1], in1=row[:],
-                op0=ALU.max, op1=ALU.mult,
-            )
+
+        def floor_and_min(i):
             nc.vector.tensor_scalar(
-                out=row[:], in0=row[:], scalar1=h_floor[:, i : i + 1], scalar2=None,
+                out=row_of[i][:], in0=row_of[i][:], scalar1=h_floor[:, i : i + 1], scalar2=None,
                 op0=ALU.max, op1=ALU.min, accum_out=h_pair[:, 0, i : i + 1],
             )
 
@@ -230,12 +242,11 @@ def tile_hyperbolicattention_kernel(tc, query, keys, values, c, out):
             )
 
         def normalise(i):
-            nc.vector.reciprocal(out=r_sum[:, i : i + 1], in_=e_sum[:, i : i + 1])
-            weights = tail.tile([P, NK], BF16, name="weights", tag="weights", bufs=GROUP)
+            weights = tail.tile([P, NK], BF16, name="weights", tag="weights", bufs=AHEAD + 1)
             weights_of[i] = weights
-            nc.gpsimd.tensor_scalar(
-                out=weights[:], in0=row_of[i][:], scalar1=r_sum[:, i : i + 1], scalar2=0.0,
-                op0=ALU.mult, op1=ALU.add,
+            nc.vector.tensor_scalar(
+                out=weights[:], in0=row_of[i][:], scalar1=r_sum[:, i : i + 1], scalar2=None,
+                op0=ALU.mult,
             )
 
         def turn_weights(i):
@@ -268,13 +279,11 @@ def tile_hyperbolicattention_kernel(tc, query, keys, values, c, out):
             nc.vector.quantize_mx(
                 out=codes[:].bitcast(FP8X4), scales=scales[:], in_=grouped_of[i][:]
             )
-            if i % 2 == 0:
-                pair = psum_out.tile([P, 2, DV], F32, name="pair", tag="pair")
-                product_of[i] = pair[:, 0, :]
-                product_of[i + 1] = pair[:, 1, :]
+            product = psum_out.tile([P, DV], F32, name="product", tag="product")
+            product_of[i] = product
             for g in range(PASSES):
                 nc.tensor.matmul_mx(
-                    out=product_of[i],
+                    out=product[:],
                     lhsT=codes[:, g * P : (g + 1) * P].bitcast(FP8X4),
                     lhsT_scale=scales[:, g * P : (g + 1) * P],
                     rhs=v_codes[:, g * DV : (g + 1) * DV].bitcast(FP8X4),
@@ -285,7 +294,7 @@ def tile_hyperbolicattention_kernel(tc, query, keys, values, c, out):
 
         def store(i):
             result = tail.tile([P, DV], F32, name="result", tag="result", bufs=GROUP)
-            nc.scalar.copy(out=result[:], in_=product_of[i])
+            nc.vector.tensor_copy(out=result[:], in_=product_of[i][:])
             nc.sync.dma_start(out=out[i * P : (i + 1) * P, :], in_=result[:])
 
         def tiles_of(g):
@@ -293,16 +302,25 @@ def tile_hyperbolicattention_kernel(tc, query, keys, values, c, out):
 
         def distance_terms(group):
             for i in group:
-                distance_term(i)
+                scaled_differences(i)
+                floor_and_min(i)
+                if i == group[0] and i + GROUP < Q_TILES:
+                    prepare_queries(i + GROUP)
             if group:
                 cols = slice(group[0], group[-1] + 1)
                 nc.vector.tensor_add(
                     out=h_pair[:, 1, cols], in0=h_pair[:, 0, cols], in1=a_q[:, cols]
                 )
 
+        def invert_sum(i):
+            nc.vector.reciprocal(out=r_sum[:, i : i + 1], in_=e_sum[:, i : i + 1])
+
         for bank in range(BANKS_PER_ROW):
             scores(0, bank)
+
         distance_terms(tiles_of(0))
+        v_codes = keep.tile([P, PASSES * DV], U32, name="v_codes", align_bytes=64)
+        v_scales = keep.tile([P, PASSES * DV], U8, name="v_scales", align_bytes=64)
         nc.vector.quantize_mx(
             out=v_codes[:].bitcast(FP8X4),
             scales=v_scales[:],
@@ -319,10 +337,10 @@ def tile_hyperbolicattention_kernel(tc, query, keys, values, c, out):
                 nc.scalar.activation(out=r_pair[:, :, cols], in_=h_pair[:, :, cols], func=ACT.Sqrt)
 
             for i in old[:AHEAD]:
+                invert_sum(i)
+            for i in old[:AHEAD]:
                 normalise(i)
-            for j in range(GROUP + 1):
-                if j + AHEAD < len(old):
-                    normalise(old[j + AHEAD])
+            for j in range(GROUP + 2):
                 if j < len(old):
                     turn_weights(old[j])
                 if j < len(cur):
@@ -334,20 +352,21 @@ def tile_hyperbolicattention_kernel(tc, query, keys, values, c, out):
                         )
                         nc.vector.reciprocal(out=inv_s_min[:, cols], in_=inv_s_min[:, cols])
                     nc.vector.tensor_add(out=row_of[i][:], in0=row_of[i][:], in1=root_of[i][:])
+                if j + AHEAD < len(old):
+                    invert_sum(old[j + AHEAD])
                 if j < len(old):
                     group_weights(old[j])
+                if j + AHEAD < len(old):
+                    normalise(old[j + AHEAD])
                 if 0 <= j - 1 < len(old):
                     quantise_and_multiply(old[j - 1])
-                    if not cur:
-                        store(old[j - 1])
+                if 0 <= j - 2 < len(old):
+                    store(old[j - 2])
 
             for i in cur:
                 nc.scalar.activation(
                     out=row_of[i][:], in_=row_of[i][:], func=ACT.Ln, scale=inv_s_min[:, i : i + 1]
                 )
-            if cur:
-                for i in old:
-                    store(i)
             distance_terms(nxt)
             for i in cur:
                 nc.scalar.activation(

@@ -91,6 +91,22 @@ def tile_hyperbolicattention_kernel(tc, query, keys, values, c, out):
         kT = keep.tile([P, D_HALVES, NK], BF16, name="kT")
         qT = keep.tile([P, D_HALVES, NQ], BF16, name="qT")
 
+        RUN = 16
+        key_squares = setup.tile([P, TURNS, D], F32, name="key_squares")
+        run_sums = setup.tile([P, TURNS, D // RUN], F32, name="run_sums")
+
+        def squared_key_norms(t0):
+            nc.scalar.activation(
+                out=key_squares[:], in_=k_nat[:, t0 : t0 + TURNS, :], func=ACT.Square
+            )
+            nc.vector.tensor_reduce(
+                out=run_sums[:], in_=key_squares[:].rearrange("p t (a b) -> p t a b", b=RUN),
+                axis=mybir.AxisListType.X, op=ALU.add,
+            )
+            nc.vector.tensor_reduce(
+                out=vv[:, t0 : t0 + TURNS], in_=run_sums[:], axis=mybir.AxisListType.X, op=ALU.add
+            )
+
         def squared_norms(nat, t0, sums):
             for t in range(t0, t0 + TURNS):
                 nc.scalar.activation(
@@ -111,7 +127,7 @@ def tile_hyperbolicattention_kernel(tc, query, keys, values, c, out):
                 )
 
         for t0 in range(0, K_TILES, TURNS):
-            squared_norms(k_nat, t0, vv)
+            squared_key_norms(t0)
             turn_features(k_nat, t0, psum_scores, "scores", nc.vector.tensor_copy, kT)
         for t0 in range(0, Q_TILES, TURNS):
             squared_norms(q_nat, t0, uu)

@@ -361,13 +361,11 @@ def tile_hyperbolicattention_kernel(tc, query, keys, values, c, out):
                     turn_weights(old[j])
                 if j < len(cur):
                     i = cur[j]
-                    if i == cur[-1]:
-                        cols = slice(cur[0], cur[-1] + 1)
-                        nc.vector.tensor_add(
-                            out=inv_s_min[:, cols], in0=r_pair[:, 0, cols], in1=r_pair[:, 1, cols]
+                    for b in range(BANKS_PER_ROW):
+                        cols = slice(b * BANK, (b + 1) * BANK)
+                        nc.gpsimd.tensor_add(
+                            out=row_of[i][:, cols], in0=row_of[i][:, cols], in1=root_of[i][:, cols]
                         )
-                        nc.vector.reciprocal(out=inv_s_min[:, cols], in_=inv_s_min[:, cols])
-                    nc.vector.tensor_add(out=row_of[i][:], in0=row_of[i][:], in1=root_of[i][:])
                 if j + AHEAD < len(old):
                     invert_sum(old[j + AHEAD])
                 if j < len(old):
@@ -379,6 +377,12 @@ def tile_hyperbolicattention_kernel(tc, query, keys, values, c, out):
                 if 0 <= j - 2 < len(old):
                     store(old[j - 2])
 
+            if cur:
+                cols = slice(cur[0], cur[-1] + 1)
+                nc.vector.tensor_add(
+                    out=inv_s_min[:, cols], in0=r_pair[:, 0, cols], in1=r_pair[:, 1, cols]
+                )
+                nc.vector.reciprocal(out=inv_s_min[:, cols], in_=inv_s_min[:, cols])
             for i in cur:
                 nc.scalar.activation(
                     out=row_of[i][:], in_=row_of[i][:], func=ACT.Ln, scale=inv_s_min[:, i : i + 1]

@@ -23,12 +23,14 @@ TURNS = BANK // P
 PACK = 4
 K_PASS = P * PACK
 PASSES = NK // K_PASS
-GROUP = 4
-N_GROUPS = Q_TILES // GROUP
+CHUNK = 4
+RUN = 16
+GROUP_SIZES = (4, 4, 4, 4)
 JUNK_SLOTS = 8
 AHEAD = 2
 
-assert GROUP == TURNS
+assert CHUNK == TURNS
+assert sum(GROUP_SIZES) == Q_TILES
 assert D_HALVES == 2
 
 FLOPS = 2 * NQ * NK * D + 2 * NQ * NK * DV
@@ -39,9 +41,8 @@ def tile_hyperbolicattention_kernel(tc, query, keys, values, c, out):
     with ExitStack() as ctx:
         ctx.enter_context(tc.manual_schedule())
         keep = ctx.enter_context(tc.tile_pool(name="keep", bufs=1))
-        setup = ctx.enter_context(tc.tile_pool(name="setup", bufs=1))
-        rows = ctx.enter_context(tc.tile_pool(name="rows", bufs=2 * GROUP))
-        roots = ctx.enter_context(tc.tile_pool(name="roots", bufs=GROUP))
+        rows = ctx.enter_context(tc.tile_pool(name="rows", bufs=12))
+        roots = ctx.enter_context(tc.tile_pool(name="roots", bufs=6))
         tail = ctx.enter_context(tc.tile_pool(name="tail", bufs=2))
         psum_scores = ctx.enter_context(tc.psum_pool(name="psum_scores", bufs=BANKS_PER_ROW))
         psum_turn = ctx.enter_context(tc.psum_pool(name="psum_turn", bufs=2))
@@ -49,13 +50,13 @@ def tile_hyperbolicattention_kernel(tc, query, keys, values, c, out):
 
         c_bf = keep.tile([P, 1], BF16, name="c_bf")
         nc.sync.dma_start(out=c_bf[:], in_=c.partition_broadcast(P))
-        k_nat = setup.tile([P, K_TILES, D], BF16, name="k_nat")
-        q_nat = setup.tile([P, Q_TILES, D], BF16, name="q_nat")
+        k_nat = rows.tile([P, K_TILES, D], BF16, name="k_nat", tag="row", align_bytes=64)
+        q_nat = rows.tile([P, Q_TILES, D], BF16, name="q_nat", tag="row", align_bytes=64)
         for nat, dram in ((k_nat, keys), (q_nat, query)):
             view = dram.rearrange("(t p) d -> p t d", p=P)
-            for t0 in range(0, K_TILES, TURNS):
-                nc.sync.dma_start(out=nat[:, t0 : t0 + TURNS, :], in_=view[:, t0 : t0 + TURNS, :])
-        v_raw = setup.tile([P, PASSES, PACK, DV], BF16, name="v_raw")
+            for t0 in range(0, K_TILES, CHUNK):
+                nc.sync.dma_start(out=nat[:, t0 : t0 + CHUNK, :], in_=view[:, t0 : t0 + CHUNK, :])
+        v_raw = rows.tile([P, PASSES, PACK, DV], BF16, name="v_raw", tag="row", align_bytes=64)
         nc.sync.dma_start(
             out=v_raw[:], in_=values.rearrange("(g p j) w -> p g j w", g=PASSES, p=P, j=PACK)
         )
@@ -85,54 +86,25 @@ def tile_hyperbolicattention_kernel(tc, query, keys, values, c, out):
             out=neg_p[:], in0=neg_p[:], scalar1=-2.0, scalar2=None, op0=ALU.mult
         )
 
-        squares = setup.tile([P, JUNK_SLOTS, D], BF16, name="squares")
-        vv = setup.tile([P, K_TILES], F32, name="vv")
-        uu = setup.tile([P, Q_TILES], F32, name="uu")
+        vv = keep.tile([P, K_TILES], F32, name="vv")
+        uu = keep.tile([P, Q_TILES], F32, name="uu")
         kT = keep.tile([P, D_HALVES, NK], BF16, name="kT")
         qT = keep.tile([P, D_HALVES, NQ], BF16, name="qT")
+        rep_vv = keep.tile([P, K_TILES, P], F32, name="rep_vv")
+        kb_neg = keep.tile([P, K_TILES], F32, name="kb_neg")
+        kb_neg_row = keep.tile([P, NK], F32, name="kb_neg_row")
 
-        RUN = 16
-        key_squares = setup.tile([P, TURNS, D], F32, name="key_squares")
-        run_sums = setup.tile([P, TURNS, D // RUN], F32, name="run_sums")
-
-        def squared_key_norms(t0):
-            nc.scalar.activation(
-                out=key_squares[:], in_=k_nat[:, t0 : t0 + TURNS, :], func=ACT.Square
-            )
-            nc.vector.tensor_reduce(
-                out=run_sums[:], in_=key_squares[:].rearrange("p t (a b) -> p t a b", b=RUN),
-                axis=mybir.AxisListType.X, op=ALU.add,
-            )
-            nc.vector.tensor_reduce(
-                out=vv[:, t0 : t0 + TURNS], in_=run_sums[:], axis=mybir.AxisListType.X, op=ALU.add
-            )
-
-        def squared_norms(nat, t0, sums):
-            for t in range(t0, t0 + TURNS):
-                nc.scalar.activation(
-                    out=squares[:, t % JUNK_SLOTS, :], in_=nat[:, t, :], func=ACT.Square,
-                    accum_out=sums[:, t : t + 1],
-                )
-
-        def turn_features(nat, t0, pool, tag, copy, dst):
+        def turn_features(nat, t0, pool, tag, copies, dst):
             for h in range(D_HALVES):
                 turned = pool.tile([P, TURNS, P], BF16, name="turned_bf", tag=tag)
                 for r in range(TURNS):
                     nc.tensor.transpose(
                         turned[:, r, :], nat[:, t0 + r, h * P : (h + 1) * P], ident_bf[:]
                     )
-                copy(
+                copies[h](
                     out=dst[:, h, t0 * P : (t0 + TURNS) * P],
                     in_=turned[:].rearrange("p r m -> p (r m)"),
                 )
-
-        for t0 in range(0, K_TILES, TURNS):
-            squared_key_norms(t0)
-            turn_features(k_nat, t0, psum_scores, "scores", nc.vector.tensor_copy, kT)
-        for t0 in range(0, Q_TILES, TURNS):
-            squared_norms(q_nat, t0, uu)
-        v_grouped = setup.tile([P, PASSES, DV, PACK], BF16, name="v_grouped", align_bytes=64)
-        nc.scalar.copy(out=v_grouped[:], in_=v_raw[:].rearrange("p g j w -> p g w j"))
 
         def one_minus_clipped(dst, sq_norms):
             nc.vector.tensor_scalar(
@@ -143,61 +115,82 @@ def tile_hyperbolicattention_kernel(tc, query, keys, values, c, out):
                 out=dst, in0=dst, scalar1=-1.0, scalar2=1.0, op0=ALU.mult, op1=ALU.add
             )
 
-        def repeat(rep, per_row):
-            nc.vector.tensor_copy(out=rep, in_=per_row.unsqueeze(2).to_broadcast(rep.shape))
-
-        def spread(row, rep):
-            turned = psum_turn.tile([P, TURNS, P], F32, name="turned_rep", tag="turn")
+        def spread(row, per_row, t0, pool, tag, copy):
+            turned = pool.tile([P, TURNS, P], F32, name="turned_col", tag=tag)
             for r in range(TURNS):
-                nc.tensor.transpose(turned[:, r, :], rep[:, r, :], ident_f32[:])
-            nc.vector.tensor_copy(out=row, in_=turned[:].rearrange("p r m -> p (r m)"))
-
-        vv_term = setup.tile([P, K_TILES], F32, name="vv_term")
-        nc.vector.tensor_scalar(
-            out=vv_term[:], in0=vv[:], scalar1=-0.5, scalar2=None, op0=ALU.mult
-        )
-        rep_vv = keep.tile([P, K_TILES, P], F32, name="rep_vv")
-        repeat(rep_vv[:], vv_term[:])
-
-        uu_term = setup.tile([P, Q_TILES], F32, name="uu_term")
-        uu_row = keep.tile([P, NQ], F32, name="uu_row")
-
-        def prepare_queries(t0):
-            turn_features(q_nat, t0, psum_turn, "turn", nc.vector.tensor_copy, qT)
-            block = slice(t0, t0 + TURNS)
-            nc.vector.tensor_scalar(
-                out=uu_term[:, block], in0=uu[:, block], scalar1=-0.5, scalar2=None, op0=ALU.mult
+                nc.tensor.transpose(
+                    turned[:, r, :], per_row[:, t0 + r : t0 + r + 1].to_broadcast([P, P]), ident_f32[:]
+                )
+            copy(
+                out=row[:, t0 * P : (t0 + TURNS) * P], in_=turned[:].rearrange("p r m -> p (r m)")
             )
-            rep_uu = tail.tile([P, TURNS, P], F32, name="rep_uu", tag="rep_uu")
-            repeat(rep_uu[:], uu_term[:, block])
-            spread(uu_row[:, t0 * P : (t0 + TURNS) * P], rep_uu)
 
-        prepare_queries(0)
+        key_squares = rows.tile([P, 2, CHUNK, D], F32, name="key_squares", tag="row", align_bytes=64)
+        run_sums = keep.tile([P, CHUNK, D // RUN], F32, name="run_sums")
+        for t0 in range(0, K_TILES, CHUNK):
+            chunk = slice(t0, t0 + CHUNK)
+            part = t0 // CHUNK % 2
+            nc.scalar.activation(
+                out=key_squares[:, part, :, :], in_=k_nat[:, chunk, :], func=ACT.Square
+            )
+            turn_features(
+                k_nat, t0, psum_scores, "scores", (nc.vector.tensor_copy, nc.scalar.copy), kT
+            )
+            nc.vector.tensor_reduce(
+                out=run_sums[:],
+                in_=key_squares[:, part, :, :].rearrange("p t (a b) -> p t a b", b=RUN),
+                axis=mybir.AxisListType.X, op=ALU.add,
+            )
+            nc.vector.tensor_reduce(
+                out=vv[:, chunk], in_=run_sums[:], axis=mybir.AxisListType.X, op=ALU.add
+            )
+            nc.gpsimd.tensor_scalar(
+                out=rep_vv[:, chunk, :], in0=vv[:, chunk].unsqueeze(2).to_broadcast([P, CHUNK, P]),
+                scalar1=-0.5, scalar2=0.0, op0=ALU.mult, op1=ALU.add,
+            )
 
-        kb_neg = setup.tile([P, K_TILES], F32, name="kb_neg")
         one_minus_clipped(kb_neg[:], vv[:])
         nc.vector.reciprocal(out=kb_neg[:], in_=kb_neg[:])
         nc.vector.tensor_scalar(
             out=kb_neg[:], in0=kb_neg[:], scalar1=kappa[:, 0:1], scalar2=-2.0,
             op0=ALU.mult, op1=ALU.mult,
         )
-        rep_kb = setup.tile([P, K_TILES, P], F32, name="rep_kb")
-        repeat(rep_kb[:], kb_neg[:])
-        kb_neg_row = keep.tile([P, NK], F32, name="kb_neg_row")
-        for t0 in range(0, K_TILES, TURNS):
-            spread(kb_neg_row[:, t0 * P : (t0 + TURNS) * P], rep_kb[:, t0 : t0 + TURNS, :])
 
+        squares = rows.tile([P, JUNK_SLOTS, D], BF16, name="squares", tag="row", align_bytes=64)
+        uu_term = keep.tile([P, Q_TILES], F32, name="uu_term")
+        uu_row = keep.tile([P, NQ], F32, name="uu_row")
         a_q = keep.tile([P, Q_TILES], F32, name="a_q")
-        one_minus_clipped(a_q[:], uu[:])
         m_neg = keep.tile([P, Q_TILES], F32, name="m_neg")
-        nc.vector.tensor_scalar(
-            out=m_neg[:], in0=a_q[:], scalar1=kappa[:, 0:1], scalar2=-2.0 / EPS,
-            op0=ALU.mult, op1=ALU.mult,
-        )
         h_floor = keep.tile([P, Q_TILES], F32, name="h_floor")
-        nc.vector.tensor_scalar(
-            out=h_floor[:], in0=a_q[:], scalar1=EPS / 2.0, scalar2=None, op0=ALU.mult
-        )
+
+        def query_norms(t0):
+            for t in range(t0, t0 + CHUNK):
+                nc.scalar.activation(
+                    out=squares[:, t % JUNK_SLOTS, :], in_=q_nat[:, t, :], func=ACT.Square,
+                    accum_out=uu[:, t : t + 1],
+                )
+
+        def prepare_queries(t0):
+            block = slice(t0, t0 + CHUNK)
+            nc.vector.tensor_scalar(
+                out=uu_term[:, block], in0=uu[:, block], scalar1=-0.5, scalar2=None, op0=ALU.mult
+            )
+            turn_features(
+                q_nat, t0, psum_turn, "turn", (nc.vector.tensor_copy, nc.vector.tensor_copy), qT
+            )
+            spread(uu_row, uu_term, t0, psum_turn, "turn", nc.vector.tensor_copy)
+            one_minus_clipped(a_q[:, block], uu[:, block])
+            nc.vector.tensor_scalar(
+                out=m_neg[:, block], in0=a_q[:, block], scalar1=kappa[:, 0:1], scalar2=-2.0 / EPS,
+                op0=ALU.mult, op1=ALU.mult,
+            )
+            nc.vector.tensor_scalar(
+                out=h_floor[:, block], in0=a_q[:, block], scalar1=EPS / 2.0, scalar2=None,
+                op0=ALU.mult,
+            )
+
+        query_norms(0)
+        prepare_queries(0)
 
         h_pair = keep.tile([P, 2, Q_TILES], F32, name="h_pair")
         r_pair = keep.tile([P, 2, Q_TILES], F32, name="r_pair")
@@ -232,7 +225,7 @@ def tile_hyperbolicattention_kernel(tc, query, keys, values, c, out):
             score_bank[(i, bank)] = ps
 
         def scaled_differences(i):
-            row = rows.tile([P, NK], F32, name="row", tag="row")
+            row = rows.tile([P, NK], F32, name="row", tag="row", align_bytes=64)
             row_of[i] = row
             for bank in range(BANKS_PER_ROW):
                 cols = slice(bank * BANK, (bank + 1) * BANK)
@@ -309,32 +302,49 @@ def tile_hyperbolicattention_kernel(tc, query, keys, values, c, out):
                 )
 
         def store(i):
-            result = tail.tile([P, DV], F32, name="result", tag="result", bufs=GROUP)
+            result = tail.tile([P, DV], F32, name="result", tag="result", bufs=4)
             nc.vector.tensor_copy(out=result[:], in_=product_of[i][:])
             nc.sync.dma_start(out=out[i * P : (i + 1) * P, :], in_=result[:])
 
-        def tiles_of(g):
-            return list(range(g * GROUP, (g + 1) * GROUP)) if 0 <= g < N_GROUPS else []
+        groups = []
+        for size in GROUP_SIZES:
+            first = sum(len(group) for group in groups)
+            groups.append(list(range(first, first + size)))
 
-        def distance_terms(group):
-            for i in group:
-                scaled_differences(i)
-                floor_and_min(i)
-                if i == group[0] and i + GROUP < Q_TILES:
-                    prepare_queries(i + GROUP)
-            if group:
-                cols = slice(group[0], group[-1] + 1)
-                nc.vector.tensor_add(
-                    out=h_pair[:, 1, cols], in0=h_pair[:, 0, cols], in1=a_q[:, cols]
-                )
+        def tiles_of(g):
+            return groups[g] if 0 <= g < len(groups) else []
+
+        def differences(i):
+            if i % CHUNK == 1 and i + CHUNK - 1 < Q_TILES:
+                prepare_queries(i + CHUNK - 1)
+            scaled_differences(i)
+
+        def finish_minima(group):
+            cols = slice(group[0], group[-1] + 1)
+            nc.vector.tensor_add(
+                out=h_pair[:, 1, cols], in0=h_pair[:, 0, cols], in1=a_q[:, cols]
+            )
 
         def invert_sum(i):
             nc.vector.reciprocal(out=r_sum[:, i : i + 1], in_=e_sum[:, i : i + 1])
 
         for bank in range(BANKS_PER_ROW):
             scores(0, bank)
+            spread(kb_neg_row, kb_neg, bank * TURNS, psum_turn, "turn", nc.scalar.copy)
+        for t0 in range(CHUNK, Q_TILES, CHUNK):
+            query_norms(t0)
 
-        distance_terms(tiles_of(0))
+        v_grouped = rows.tile([P, PASSES, DV, PACK], BF16, name="v_grouped", tag="row", align_bytes=64)
+        for g in range(PASSES):
+            nc.gpsimd.tensor_scalar(
+                out=v_grouped[:, g, :, :], in0=v_raw[:, g, :, :].rearrange("p j w -> p w j"),
+                scalar1=1.0, scalar2=0.0, op0=ALU.mult, op1=ALU.add,
+            )
+
+        for i in groups[0]:
+            differences(i)
+            floor_and_min(i)
+        finish_minima(groups[0])
         v_codes = keep.tile([P, PASSES * DV], U32, name="v_codes", align_bytes=64)
         v_scales = keep.tile([P, PASSES * DV], U8, name="v_scales", align_bytes=64)
         nc.vector.quantize_mx(
@@ -343,51 +353,54 @@ def tile_hyperbolicattention_kernel(tc, query, keys, values, c, out):
             in_=v_grouped[:].rearrange("p g w j -> p (g w j)"),
         )
 
-        for g in range(N_GROUPS + 1):
+        for g in range(len(groups) + 1):
             cur, old, nxt = tiles_of(g), tiles_of(g - 1), tiles_of(g + 1)
-
             for i in cur:
+                if i == cur[-1]:
+                    cols = slice(cur[0], cur[-1] + 1)
+                    nc.scalar.activation(
+                        out=r_pair[:, :, cols], in_=h_pair[:, :, cols], func=ACT.Sqrt
+                    )
                 square_roots(i)
-            if cur:
-                cols = slice(cur[0], cur[-1] + 1)
-                nc.scalar.activation(out=r_pair[:, :, cols], in_=h_pair[:, :, cols], func=ACT.Sqrt)
+                for bank in range(BANKS_PER_ROW):
+                    part = slice(bank * BANK, (bank + 1) * BANK)
+                    nc.gpsimd.tensor_add(
+                        out=row_of[i][:, part], in0=row_of[i][:, part], in1=root_of[i][:, part]
+                    )
 
             for i in old[:AHEAD]:
                 invert_sum(i)
             for i in old[:AHEAD]:
                 normalise(i)
-            for j in range(GROUP + 2):
+            for j in range(max(len(old) + 2, len(nxt))):
+                if j < len(nxt):
+                    differences(nxt[j])
                 if j < len(old):
                     turn_weights(old[j])
-                if j < len(cur):
-                    i = cur[j]
-                    for b in range(BANKS_PER_ROW):
-                        cols = slice(b * BANK, (b + 1) * BANK)
-                        nc.gpsimd.tensor_add(
-                            out=row_of[i][:, cols], in0=row_of[i][:, cols], in1=root_of[i][:, cols]
-                        )
                 if j + AHEAD < len(old):
                     invert_sum(old[j + AHEAD])
                 if j < len(old):
                     group_weights(old[j])
+                if j < len(nxt):
+                    floor_and_min(nxt[j])
+                if j == 1 and cur:
+                    nc.vector.tensor_add(
+                        out=inv_s_min[:, cols], in0=r_pair[:, 0, cols], in1=r_pair[:, 1, cols]
+                    )
+                    nc.vector.reciprocal(out=inv_s_min[:, cols], in_=inv_s_min[:, cols])
                 if j + AHEAD < len(old):
                     normalise(old[j + AHEAD])
+                if j < len(old):
+                    quantise_and_multiply(old[j])
                 if 0 <= j - 1 < len(old):
-                    quantise_and_multiply(old[j - 1])
-                if 0 <= j - 2 < len(old):
-                    store(old[j - 2])
+                    store(old[j - 1])
+            if nxt:
+                finish_minima(nxt)
 
-            if cur:
-                cols = slice(cur[0], cur[-1] + 1)
-                nc.vector.tensor_add(
-                    out=inv_s_min[:, cols], in0=r_pair[:, 0, cols], in1=r_pair[:, 1, cols]
-                )
-                nc.vector.reciprocal(out=inv_s_min[:, cols], in_=inv_s_min[:, cols])
             for i in cur:
                 nc.scalar.activation(
                     out=row_of[i][:], in_=row_of[i][:], func=ACT.Ln, scale=inv_s_min[:, i : i + 1]
                 )
-            distance_terms(nxt)
             for i in cur:
                 nc.scalar.activation(
                     out=row_of[i][:], in_=row_of[i][:], func=ACT.Exp, scale=neg_p[:, 0:1],

@@ -27,7 +27,6 @@ CHUNK = 4
 RUN = 16
 GROUP_SIZES = (4, 4, 4, 4)
 JUNK_SLOTS = 8
-AHEAD = 2
 
 assert CHUNK == TURNS
 assert sum(GROUP_SIZES) == Q_TILES
@@ -251,7 +250,7 @@ def tile_hyperbolicattention_kernel(tc, query, keys, values, c, out):
             )
 
         def normalise(i):
-            weights = tail.tile([P, NK], BF16, name="weights", tag="weights", bufs=AHEAD + 1)
+            weights = tail.tile([P, NK], BF16, name="weights", tag="weights")
             weights_of[i] = weights
             nc.vector.tensor_scalar(
                 out=weights[:], in0=row_of[i][:], scalar1=r_sum[:, i : i + 1], scalar2=None,
@@ -314,10 +313,9 @@ def tile_hyperbolicattention_kernel(tc, query, keys, values, c, out):
         def tiles_of(g):
             return groups[g] if 0 <= g < len(groups) else []
 
-        def differences(i):
+        def prepare_ahead(i):
             if i % CHUNK == 1 and i + CHUNK - 1 < Q_TILES:
                 prepare_queries(i + CHUNK - 1)
-            scaled_differences(i)
 
         def finish_minima(group):
             cols = slice(group[0], group[-1] + 1)
@@ -342,7 +340,8 @@ def tile_hyperbolicattention_kernel(tc, query, keys, values, c, out):
             )
 
         for i in groups[0]:
-            differences(i)
+            prepare_ahead(i)
+            scaled_differences(i)
             floor_and_min(i)
         finish_minima(groups[0])
         v_codes = keep.tile([P, PASSES * DV], U32, name="v_codes", align_bytes=64)
@@ -356,7 +355,7 @@ def tile_hyperbolicattention_kernel(tc, query, keys, values, c, out):
         for g in range(len(groups) + 1):
             cur, old, nxt = tiles_of(g), tiles_of(g - 1), tiles_of(g + 1)
             for i in cur:
-                if i == cur[-1]:
+                if i == (cur[-1] if g == 0 else cur[0]):
                     cols = slice(cur[0], cur[-1] + 1)
                     nc.scalar.activation(
                         out=r_pair[:, :, cols], in_=h_pair[:, :, cols], func=ACT.Sqrt
@@ -368,32 +367,34 @@ def tile_hyperbolicattention_kernel(tc, query, keys, values, c, out):
                         out=row_of[i][:, part], in0=row_of[i][:, part], in1=root_of[i][:, part]
                     )
 
-            for i in old[:AHEAD]:
-                invert_sum(i)
-            for i in old[:AHEAD]:
-                normalise(i)
-            for j in range(max(len(old) + 2, len(nxt))):
+            if old:
+                invert_sum(old[0])
+                normalise(old[0])
+                turn_weights(old[0])
+            for j in range(max(len(old) + 1, len(nxt))):
+                if j + 1 < len(old):
+                    invert_sum(old[j + 1])
                 if j < len(nxt):
-                    differences(nxt[j])
-                if j < len(old):
-                    turn_weights(old[j])
-                if j + AHEAD < len(old):
-                    invert_sum(old[j + AHEAD])
+                    scaled_differences(nxt[j])
+                if j + 1 < len(old):
+                    normalise(old[j + 1])
                 if j < len(old):
                     group_weights(old[j])
                 if j < len(nxt):
+                    prepare_ahead(nxt[j])
+                if j + 1 < len(old):
+                    turn_weights(old[j + 1])
+                if j < len(nxt):
                     floor_and_min(nxt[j])
-                if j == 1 and cur:
+                if j == 0 and cur:
                     nc.vector.tensor_add(
                         out=inv_s_min[:, cols], in0=r_pair[:, 0, cols], in1=r_pair[:, 1, cols]
                     )
                     nc.vector.reciprocal(out=inv_s_min[:, cols], in_=inv_s_min[:, cols])
-                if j + AHEAD < len(old):
-                    normalise(old[j + AHEAD])
-                if j < len(old):
-                    quantise_and_multiply(old[j])
                 if 0 <= j - 1 < len(old):
                     store(old[j - 1])
+                if j < len(old):
+                    quantise_and_multiply(old[j])
             if nxt:
                 finish_minima(nxt)
 

@@ -19,6 +19,7 @@ K_TILES = NK // P
 D_HALVES = D // P
 BANK = 512
 BANKS_PER_ROW = NK // BANK
+BANK_HALVES = ((0, 1), (2, 3))
 TURNS = BANK // P
 PACK = 4
 K_PASS = P * PACK
@@ -205,35 +206,40 @@ def tile_hyperbolicattention_kernel(tc, query, keys, values, c, out):
         grouped_of = {}
         product_of = {}
 
-        def scores(i, bank):
-            ps = psum_scores.tile([P, BANK], F32, name="ps", tag="scores")
+        def scores(i, banks):
             queries = slice(i * P, (i + 1) * P)
-            keys_of_bank = slice(bank * BANK, (bank + 1) * BANK)
-            nc.tensor.matmul(
-                ps[:], lhsT=qT[:, 0, queries], rhs=kT[:, 0, keys_of_bank], start=True, stop=False
-            )
-            for r in range(TURNS):
-                for term in (rep_vv[:, bank * TURNS + r, :], uu_row[:, queries]):
-                    nc.tensor.matmul(
-                        ps[:, r * P : (r + 1) * P], lhsT=term, rhs=ident_f32[:],
-                        is_transpose=True, start=False, stop=False,
-                    )
-            nc.tensor.matmul(
-                ps[:], lhsT=qT[:, 1, queries], rhs=kT[:, 1, keys_of_bank], start=False, stop=True
-            )
-            score_bank[(i, bank)] = ps
+            for bank in banks:
+                ps = psum_scores.tile([P, BANK], F32, name="ps", tag="scores")
+                score_bank[(i, bank)] = ps
+                nc.tensor.matmul(
+                    ps[:], lhsT=qT[:, 0, queries], rhs=kT[:, 0, bank * BANK : (bank + 1) * BANK],
+                    start=True, stop=False,
+                )
+            for bank in banks:
+                for r in range(TURNS):
+                    for term in (rep_vv[:, bank * TURNS + r, :], uu_row[:, queries]):
+                        nc.tensor.matmul(
+                            score_bank[(i, bank)][:, r * P : (r + 1) * P], lhsT=term,
+                            rhs=ident_f32[:], is_transpose=True, start=False, stop=False,
+                        )
+            for bank in banks:
+                nc.tensor.matmul(
+                    score_bank[(i, bank)][:], lhsT=qT[:, 1, queries],
+                    rhs=kT[:, 1, bank * BANK : (bank + 1) * BANK], start=False, stop=True,
+                )
 
         def scaled_differences(i):
             row = rows.tile([P, NK], F32, name="row", tag="row", align_bytes=64)
             row_of[i] = row
-            for bank in range(BANKS_PER_ROW):
-                cols = slice(bank * BANK, (bank + 1) * BANK)
-                nc.vector.scalar_tensor_tensor(
-                    out=row[:, cols], in0=kb_neg_row[:, cols], scalar=m_neg[:, i : i + 1],
-                    in1=score_bank[(i, bank)][:], op0=ALU.max, op1=ALU.mult,
-                )
+            for banks in BANK_HALVES:
+                for bank in banks:
+                    cols = slice(bank * BANK, (bank + 1) * BANK)
+                    nc.vector.scalar_tensor_tensor(
+                        out=row[:, cols], in0=kb_neg_row[:, cols], scalar=m_neg[:, i : i + 1],
+                        in1=score_bank[(i, bank)][:], op0=ALU.max, op1=ALU.mult,
+                    )
                 if i + 1 < Q_TILES:
-                    scores(i + 1, bank)
+                    scores(i + 1, banks)
 
         def floor_and_min(i):
             nc.vector.tensor_scalar(
@@ -326,8 +332,9 @@ def tile_hyperbolicattention_kernel(tc, query, keys, values, c, out):
         def invert_sum(i):
             nc.vector.reciprocal(out=r_sum[:, i : i + 1], in_=e_sum[:, i : i + 1])
 
+        for banks in BANK_HALVES:
+            scores(0, banks)
         for bank in range(BANKS_PER_ROW):
-            scores(0, bank)
             spread(kb_neg_row, kb_neg, bank * TURNS, psum_turn, "turn", nc.scalar.copy)
         for t0 in range(CHUNK, Q_TILES, CHUNK):
             query_norms(t0)

@@ -26,7 +26,7 @@ K_PASS = P * PACK
 PASSES = NK // K_PASS
 CHUNK = 4
 RUN = 16
-GROUP_SIZES = (4, 4, 4, 4)
+GROUP_SIZES = (5, 5, 6)
 JUNK_SLOTS = 8
 
 assert CHUNK == TURNS
@@ -41,8 +41,7 @@ def tile_hyperbolicattention_kernel(tc, query, keys, values, c, out):
     with ExitStack() as ctx:
         ctx.enter_context(tc.manual_schedule())
         keep = ctx.enter_context(tc.tile_pool(name="keep", bufs=1))
-        rows = ctx.enter_context(tc.tile_pool(name="rows", bufs=12))
-        roots = ctx.enter_context(tc.tile_pool(name="roots", bufs=6))
+        rows = ctx.enter_context(tc.tile_pool(name="rows", bufs=20))
         tail = ctx.enter_context(tc.tile_pool(name="tail", bufs=2))
         psum_scores = ctx.enter_context(tc.psum_pool(name="psum_scores", bufs=BANKS_PER_ROW))
         psum_turn = ctx.enter_context(tc.psum_pool(name="psum_turn", bufs=2))
@@ -52,10 +51,14 @@ def tile_hyperbolicattention_kernel(tc, query, keys, values, c, out):
         nc.sync.dma_start(out=c_bf[:], in_=c.partition_broadcast(P))
         k_nat = rows.tile([P, K_TILES, D], BF16, name="k_nat", tag="row", align_bytes=64)
         q_nat = rows.tile([P, Q_TILES, D], BF16, name="q_nat", tag="row", align_bytes=64)
-        for nat, dram in ((k_nat, keys), (q_nat, query)):
-            view = dram.rearrange("(t p) d -> p t d", p=P)
-            for t0 in range(0, K_TILES, CHUNK):
-                nc.sync.dma_start(out=nat[:, t0 : t0 + CHUNK, :], in_=view[:, t0 : t0 + CHUNK, :])
+        k_view = keys.rearrange("(t p) d -> p t d", p=P)
+        q_view = query.rearrange("(t p) d -> p t d", p=P)
+        for nat, view, chunk in (
+            (k_nat, k_view, 0), (q_nat, q_view, 0), (k_nat, k_view, 1), (k_nat, k_view, 2),
+            (k_nat, k_view, 3), (q_nat, q_view, 1), (q_nat, q_view, 2), (q_nat, q_view, 3),
+        ):
+            tiles = slice(chunk * CHUNK, (chunk + 1) * CHUNK)
+            nc.sync.dma_start(out=nat[:, tiles, :], in_=view[:, tiles, :])
         v_raw = rows.tile([P, PASSES, PACK, DV], BF16, name="v_raw", tag="row", align_bytes=64)
         nc.sync.dma_start(
             out=v_raw[:], in_=values.rearrange("(g p j) w -> p g j w", g=PASSES, p=P, j=PACK)
@@ -84,6 +87,10 @@ def tile_hyperbolicattention_kernel(tc, query, keys, values, c, out):
         nc.vector.reciprocal(out=neg_p[:], in_=neg_p[:])
         nc.vector.tensor_scalar(
             out=neg_p[:], in0=neg_p[:], scalar1=-2.0, scalar2=None, op0=ALU.mult
+        )
+        neg_half_p = keep.tile([P, 1], F32, name="neg_half_p")
+        nc.vector.tensor_scalar(
+            out=neg_half_p[:], in0=neg_p[:], scalar1=0.5, scalar2=None, op0=ALU.mult
         )
 
         vv = keep.tile([P, K_TILES], F32, name="vv")
@@ -125,9 +132,63 @@ def tile_hyperbolicattention_kernel(tc, query, keys, values, c, out):
                 out=row[:, t0 * P : (t0 + TURNS) * P], in_=turned[:].rearrange("p r m -> p (r m)")
             )
 
+        squares = rows.tile([P, JUNK_SLOTS, D], BF16, name="squares", tag="row", align_bytes=64)
+        uu_term = keep.tile([P, Q_TILES], F32, name="uu_term")
+        uu_row = keep.tile([P, NQ], F32, name="uu_row")
+        a_q = keep.tile([P, Q_TILES], F32, name="a_q")
+        m_neg = keep.tile([P, Q_TILES], F32, name="m_neg")
+        h_floor = keep.tile([P, Q_TILES], F32, name="h_floor")
+
+        def query_norms(t0):
+            for t in range(t0, t0 + CHUNK):
+                nc.scalar.activation(
+                    out=squares[:, t % JUNK_SLOTS, :], in_=q_nat[:, t, :], func=ACT.Square,
+                    accum_out=uu[:, t : t + 1],
+                )
+
+        def query_terms(tiles):
+            nc.vector.tensor_scalar(
+                out=uu_term[:, tiles], in0=uu[:, tiles], scalar1=-0.5, scalar2=None, op0=ALU.mult
+            )
+            one_minus_clipped(a_q[:, tiles], uu[:, tiles])
+            nc.vector.tensor_scalar(
+                out=m_neg[:, tiles], in0=a_q[:, tiles], scalar1=kappa[:, 0:1], scalar2=-2.0 / EPS,
+                op0=ALU.mult, op1=ALU.mult,
+            )
+            nc.vector.tensor_scalar(
+                out=h_floor[:, tiles], in0=a_q[:, tiles], scalar1=EPS / 2.0, scalar2=None,
+                op0=ALU.mult,
+            )
+
+        def turn_queries(t0):
+            features = psum_out.tile([P, D_HALVES, TURNS, P], BF16, name="turned_q", tag="product")
+            for h in range(D_HALVES):
+                for r in range(TURNS):
+                    nc.tensor.transpose(
+                        features[:, h, r, :], q_nat[:, t0 + r, h * P : (h + 1) * P], ident_bf[:]
+                    )
+            norms = psum_out.tile([P, TURNS, P], F32, name="turned_uu", tag="product")
+            for r in range(TURNS):
+                nc.tensor.transpose(
+                    norms[:, r, :], uu_term[:, t0 + r : t0 + r + 1].to_broadcast([P, P]), ident_f32[:]
+                )
+
+            def take():
+                queries = slice(t0 * P, (t0 + TURNS) * P)
+                for h in range(D_HALVES):
+                    nc.vector.tensor_copy(
+                        out=qT[:, h, queries], in_=features[:, h, :, :].rearrange("p r m -> p (r m)")
+                    )
+                nc.vector.tensor_copy(
+                    out=uu_row[:, queries], in_=norms[:].rearrange("p r m -> p (r m)")
+                )
+
+            return take
+
         key_squares = rows.tile([P, 2, CHUNK, D], F32, name="key_squares", tag="row", align_bytes=64)
         run_sums = keep.tile([P, CHUNK, D // RUN], F32, name="run_sums")
-        for t0 in range(0, K_TILES, CHUNK):
+
+        def prepare_keys(t0):
             chunk = slice(t0, t0 + CHUNK)
             part = t0 // CHUNK % 2
             nc.scalar.activation(
@@ -149,52 +210,32 @@ def tile_hyperbolicattention_kernel(tc, query, keys, values, c, out):
                 scalar1=-0.5, scalar2=0.0, op0=ALU.mult, op1=ALU.add,
             )
 
-        one_minus_clipped(kb_neg[:], vv[:])
-        nc.vector.reciprocal(out=kb_neg[:], in_=kb_neg[:])
-        nc.vector.tensor_scalar(
-            out=kb_neg[:], in0=kb_neg[:], scalar1=kappa[:, 0:1], scalar2=-2.0,
-            op0=ALU.mult, op1=ALU.mult,
-        )
-
-        squares = rows.tile([P, JUNK_SLOTS, D], BF16, name="squares", tag="row", align_bytes=64)
-        uu_term = keep.tile([P, Q_TILES], F32, name="uu_term")
-        uu_row = keep.tile([P, NQ], F32, name="uu_row")
-        a_q = keep.tile([P, Q_TILES], F32, name="a_q")
-        m_neg = keep.tile([P, Q_TILES], F32, name="m_neg")
-        h_floor = keep.tile([P, Q_TILES], F32, name="h_floor")
-
-        def query_norms(t0):
-            for t in range(t0, t0 + CHUNK):
-                nc.scalar.activation(
-                    out=squares[:, t % JUNK_SLOTS, :], in_=q_nat[:, t, :], func=ACT.Square,
-                    accum_out=uu[:, t : t + 1],
-                )
-
-        def prepare_queries(t0):
-            block = slice(t0, t0 + CHUNK)
+        def key_factors(tiles):
+            one_minus_clipped(kb_neg[:, tiles], vv[:, tiles])
+            nc.vector.reciprocal(out=kb_neg[:, tiles], in_=kb_neg[:, tiles])
             nc.vector.tensor_scalar(
-                out=uu_term[:, block], in0=uu[:, block], scalar1=-0.5, scalar2=None, op0=ALU.mult
-            )
-            turn_features(
-                q_nat, t0, psum_turn, "turn", (nc.vector.tensor_copy, nc.vector.tensor_copy), qT
-            )
-            spread(uu_row, uu_term, t0, psum_turn, "turn", nc.vector.tensor_copy)
-            one_minus_clipped(a_q[:, block], uu[:, block])
-            nc.vector.tensor_scalar(
-                out=m_neg[:, block], in0=a_q[:, block], scalar1=kappa[:, 0:1], scalar2=-2.0 / EPS,
+                out=kb_neg[:, tiles], in0=kb_neg[:, tiles], scalar1=kappa[:, 0:1], scalar2=-2.0,
                 op0=ALU.mult, op1=ALU.mult,
             )
-            nc.vector.tensor_scalar(
-                out=h_floor[:, block], in0=a_q[:, block], scalar1=EPS / 2.0, scalar2=None,
-                op0=ALU.mult,
-            )
 
+        prepare_keys(0)
         query_norms(0)
-        prepare_queries(0)
+        query_terms(slice(0, CHUNK))
+        turn_features(
+            q_nat, 0, psum_turn, "turn", (nc.vector.tensor_copy, nc.vector.tensor_copy), qT
+        )
+        prepare_keys(CHUNK)
+        spread(uu_row, uu_term, 0, psum_turn, "turn", nc.vector.tensor_copy)
+        key_factors(slice(0, 2 * CHUNK))
+        prepare_keys(2 * CHUNK)
+        prepare_keys(3 * CHUNK)
+        key_factors(slice(2 * CHUNK, K_TILES))
 
         h_pair = keep.tile([P, 2, Q_TILES], F32, name="h_pair")
         r_pair = keep.tile([P, 2, Q_TILES], F32, name="r_pair")
         inv_s_min = keep.tile([P, Q_TILES], F32, name="inv_s_min")
+        inv_s_min_sq = keep.tile([P, Q_TILES], F32, name="inv_s_min_sq")
+        shift = keep.tile([P, Q_TILES], F32, name="shift")
         e_sum = keep.tile([P, Q_TILES], F32, name="e_sum")
         r_sum = keep.tile([P, Q_TILES], F32, name="r_sum")
 
@@ -247,8 +288,25 @@ def tile_hyperbolicattention_kernel(tc, query, keys, values, c, out):
                 op0=ALU.max, op1=ALU.min, accum_out=h_pair[:, 0, i : i + 1],
             )
 
+        def has_one_root(i):
+            return i >= 12
+
+        def adds_on_vector(i):
+            return i >= 14
+
+        def product_under_root(i):
+            root = rows.tile([P, NK], F32, name="root", tag="row", align_bytes=64)
+            root_of[i] = root
+            nc.vector.scalar_tensor_tensor(
+                out=root[:], in0=row_of[i][:], scalar=a_q[:, i : i + 1], in1=row_of[i][:],
+                op0=ALU.add, op1=ALU.mult,
+            )
+
         def square_roots(i):
-            root = roots.tile([P, NK], F32, name="root", tag="root")
+            if has_one_root(i):
+                nc.scalar.activation(out=root_of[i][:], in_=root_of[i][:], func=ACT.Sqrt)
+                return
+            root = rows.tile([P, NK], F32, name="root", tag="row", align_bytes=64)
             root_of[i] = root
             nc.scalar.activation(out=root[:], in_=row_of[i][:], func=ACT.Sqrt)
             nc.scalar.activation(
@@ -319,9 +377,14 @@ def tile_hyperbolicattention_kernel(tc, query, keys, values, c, out):
         def tiles_of(g):
             return groups[g] if 0 <= g < len(groups) else []
 
-        def prepare_ahead(i):
-            if i % CHUNK == 1 and i + CHUNK - 1 < Q_TILES:
-                prepare_queries(i + CHUNK - 1)
+        def distance_terms(i):
+            t0 = i + CHUNK - 1
+            preparing = i % CHUNK == 1 and t0 < Q_TILES
+            if preparing:
+                take = turn_queries(t0)
+            scaled_differences(i)
+            if preparing:
+                take()
 
         def finish_minima(group):
             cols = slice(group[0], group[-1] + 1)
@@ -329,13 +392,47 @@ def tile_hyperbolicattention_kernel(tc, query, keys, values, c, out):
                 out=h_pair[:, 1, cols], in0=h_pair[:, 0, cols], in1=a_q[:, cols]
             )
 
+        def minimum_terms(group):
+            cols = slice(group[0], group[-1] + 1)
+            nc.vector.tensor_add(
+                out=inv_s_min[:, cols], in0=r_pair[:, 0, cols], in1=r_pair[:, 1, cols]
+            )
+            nc.vector.reciprocal(out=inv_s_min[:, cols], in_=inv_s_min[:, cols])
+            nc.vector.tensor_mul(
+                out=shift[:, cols], in0=inv_s_min[:, cols], in1=inv_s_min[:, cols]
+            )
+            nc.vector.tensor_scalar(
+                out=inv_s_min_sq[:, cols], in0=shift[:, cols], scalar1=2.0, scalar2=None,
+                op0=ALU.mult,
+            )
+            nc.vector.tensor_mul(out=shift[:, cols], in0=shift[:, cols], in1=a_q[:, cols])
+
+        def logarithm(i):
+            col = slice(i, i + 1)
+            if has_one_root(i):
+                nc.scalar.activation(
+                    out=row_of[i][:], in_=row_of[i][:], func=ACT.Ln,
+                    scale=inv_s_min_sq[:, col], bias=shift[:, col],
+                )
+            else:
+                nc.scalar.activation(
+                    out=row_of[i][:], in_=row_of[i][:], func=ACT.Ln, scale=inv_s_min[:, col]
+                )
+
+        def exponential(i):
+            power = neg_half_p if has_one_root(i) else neg_p
+            nc.scalar.activation(
+                out=row_of[i][:], in_=row_of[i][:], func=ACT.Exp, scale=power[:, 0:1],
+                accum_out=e_sum[:, i : i + 1],
+            )
+
         def invert_sum(i):
             nc.vector.reciprocal(out=r_sum[:, i : i + 1], in_=e_sum[:, i : i + 1])
 
         for banks in BANK_HALVES:
+            for bank in banks:
+                spread(kb_neg_row, kb_neg, bank * TURNS, psum_turn, "turn", nc.scalar.copy)
             scores(0, banks)
-        for bank in range(BANKS_PER_ROW):
-            spread(kb_neg_row, kb_neg, bank * TURNS, psum_turn, "turn", nc.scalar.copy)
         for t0 in range(CHUNK, Q_TILES, CHUNK):
             query_norms(t0)
 
@@ -346,11 +443,28 @@ def tile_hyperbolicattention_kernel(tc, query, keys, values, c, out):
                 scalar1=1.0, scalar2=0.0, op0=ALU.mult, op1=ALU.add,
             )
 
+        def root_minima(group):
+            cols = slice(group[0], group[-1] + 1)
+            nc.scalar.activation(out=r_pair[:, :, cols], in_=h_pair[:, :, cols], func=ACT.Sqrt)
+
+        def add_roots(i):
+            for bank in range(0 if adds_on_vector(i) else BANKS_PER_ROW):
+                part = slice(bank * BANK, (bank + 1) * BANK)
+                nc.gpsimd.tensor_add(
+                    out=row_of[i][:, part], in0=row_of[i][:, part], in1=root_of[i][:, part]
+                )
+
         for i in groups[0]:
-            prepare_ahead(i)
-            scaled_differences(i)
+            if i == 1:
+                query_terms(slice(CHUNK, Q_TILES))
+            distance_terms(i)
             floor_and_min(i)
-        finish_minima(groups[0])
+            if i == groups[0][-1]:
+                finish_minima(groups[0])
+                root_minima(groups[0])
+            square_roots(i)
+            add_roots(i)
+
         v_codes = keep.tile([P, PASSES * DV], U32, name="v_codes", align_bytes=64)
         v_scales = keep.tile([P, PASSES * DV], U8, name="v_scales", align_bytes=64)
         nc.vector.quantize_mx(
@@ -361,18 +475,15 @@ def tile_hyperbolicattention_kernel(tc, query, keys, values, c, out):
 
         for g in range(len(groups) + 1):
             cur, old, nxt = tiles_of(g), tiles_of(g - 1), tiles_of(g + 1)
-            for i in cur:
-                if i == (cur[-1] if g == 0 else cur[0]):
-                    cols = slice(cur[0], cur[-1] + 1)
-                    nc.scalar.activation(
-                        out=r_pair[:, :, cols], in_=h_pair[:, :, cols], func=ACT.Sqrt
-                    )
-                square_roots(i)
-                for bank in range(BANKS_PER_ROW):
-                    part = slice(bank * BANK, (bank + 1) * BANK)
-                    nc.gpsimd.tensor_add(
-                        out=row_of[i][:, part], in0=row_of[i][:, part], in1=root_of[i][:, part]
-                    )
+            if g == 0:
+                minimum_terms(cur)
+            if cur and g > 0:
+                root_minima(cur)
+                for i in cur:
+                    if has_one_root(i):
+                        product_under_root(i)
+                    square_roots(i)
+                    add_roots(i)
 
             if old:
                 invert_sum(old[0])
@@ -382,35 +493,30 @@ def tile_hyperbolicattention_kernel(tc, query, keys, values, c, out):
                 if j + 1 < len(old):
                     invert_sum(old[j + 1])
                 if j < len(nxt):
-                    scaled_differences(nxt[j])
+                    distance_terms(nxt[j])
                 if j + 1 < len(old):
                     normalise(old[j + 1])
                 if j < len(old):
                     group_weights(old[j])
-                if j < len(nxt):
-                    prepare_ahead(nxt[j])
                 if j + 1 < len(old):
                     turn_weights(old[j + 1])
                 if j < len(nxt):
                     floor_and_min(nxt[j])
-                if j == 0 and cur:
-                    nc.vector.tensor_add(
-                        out=inv_s_min[:, cols], in0=r_pair[:, 0, cols], in1=r_pair[:, 1, cols]
-                    )
-                    nc.vector.reciprocal(out=inv_s_min[:, cols], in_=inv_s_min[:, cols])
-                if 0 <= j - 1 < len(old):
-                    store(old[j - 1])
+                if j == 0 and cur and g > 0:
+                    minimum_terms(cur)
+                for i in cur:
+                    if adds_on_vector(i) and j == i - 13:
+                        nc.vector.tensor_add(
+                            out=row_of[i][:], in0=row_of[i][:], in1=root_of[i][:]
+                        )
                 if j < len(old):
                     quantise_and_multiply(old[j])
+                if 0 <= j - 1 < len(old):
+                    store(old[j - 1])
             if nxt:
                 finish_minima(nxt)
 
             for i in cur:
-                nc.scalar.activation(
-                    out=row_of[i][:], in_=row_of[i][:], func=ACT.Ln, scale=inv_s_min[:, i : i + 1]
-                )
+                logarithm(i)
             for i in cur:
-                nc.scalar.activation(
-                    out=row_of[i][:], in_=row_of[i][:], func=ACT.Exp, scale=neg_p[:, 0:1],
-                    accum_out=e_sum[:, i : i + 1],
-                )
+                exponential(i)

@@ -27,6 +27,7 @@ PASSES = NK // K_PASS
 CHUNK = 4
 RUN = 16
 GROUP_SIZES = (5, 5, 6)
+ADD_PIECES = 2
 JUNK_SLOTS = 8
 
 assert CHUNK == TURNS
@@ -41,7 +42,7 @@ def tile_hyperbolicattention_kernel(tc, query, keys, values, c, out):
     with ExitStack() as ctx:
         ctx.enter_context(tc.manual_schedule())
         keep = ctx.enter_context(tc.tile_pool(name="keep", bufs=1))
-        rows = ctx.enter_context(tc.tile_pool(name="rows", bufs=20))
+        rows = ctx.enter_context(tc.tile_pool(name="rows", bufs=19))
         tail = ctx.enter_context(tc.tile_pool(name="tail", bufs=2))
         psum_scores = ctx.enter_context(tc.psum_pool(name="psum_scores", bufs=BANKS_PER_ROW))
         psum_turn = ctx.enter_context(tc.psum_pool(name="psum_turn", bufs=2))
@@ -289,18 +290,32 @@ def tile_hyperbolicattention_kernel(tc, query, keys, values, c, out):
             )
 
         def has_one_root(i):
-            return i >= 12
+            return i in (5, 6) or i >= 12
+
+        def product_on_gpsimd(i):
+            return i in (5, 6)
 
         def adds_on_vector(i):
-            return i >= 14
+            return i >= 13
 
         def product_under_root(i):
             root = rows.tile([P, NK], F32, name="root", tag="row", align_bytes=64)
             root_of[i] = root
-            nc.vector.scalar_tensor_tensor(
-                out=root[:], in0=row_of[i][:], scalar=a_q[:, i : i + 1], in1=row_of[i][:],
-                op0=ALU.add, op1=ALU.mult,
-            )
+            if product_on_gpsimd(i):
+                for piece in range(1):
+                    part = slice(piece * NK // 1, (piece + 1) * NK // 1)
+                    nc.gpsimd.tensor_scalar(
+                        out=root[:, part], in0=row_of[i][:, part], scalar1=a_q[:, i : i + 1],
+                        scalar2=1.0, op0=ALU.add, op1=ALU.mult,
+                    )
+                    nc.gpsimd.tensor_mul(
+                        out=root[:, part], in0=root[:, part], in1=row_of[i][:, part]
+                    )
+            else:
+                nc.vector.scalar_tensor_tensor(
+                    out=root[:], in0=row_of[i][:], scalar=a_q[:, i : i + 1], in1=row_of[i][:],
+                    op0=ALU.add, op1=ALU.mult,
+                )
 
         def square_roots(i):
             if has_one_root(i):
@@ -314,11 +329,13 @@ def tile_hyperbolicattention_kernel(tc, query, keys, values, c, out):
             )
 
         def normalise(i):
-            weights = tail.tile([P, NK], BF16, name="weights", tag="weights")
+            weights = tail.tile([P, NK], BF16, name="weights", tag="weights", bufs=4)
             weights_of[i] = weights
-            nc.vector.tensor_scalar(
-                out=weights[:], in0=row_of[i][:], scalar1=r_sum[:, i : i + 1], scalar2=None,
-                op0=ALU.mult,
+            engine = nc.gpsimd if i in (0, 1, 2, 3, 5, 6, 7, 12, 14) else nc.vector
+            nc.vector.reciprocal(out=r_sum[:, i : i + 1], in_=e_sum[:, i : i + 1])
+            engine.tensor_scalar(
+                out=weights[:], in0=row_of[i][:], scalar1=r_sum[:, i : i + 1], scalar2=0.0,
+                op0=ALU.mult, op1=ALU.add,
             )
 
         def turn_weights(i):
@@ -339,8 +356,9 @@ def tile_hyperbolicattention_kernel(tc, query, keys, values, c, out):
             grouped = tail.tile([P, NK], BF16, name="grouped", tag="grouped", align_bytes=64)
             grouped_of[i] = grouped
             words = grouped[:].bitcast(F32).rearrange("p (g q u) -> p g q u", g=PASSES, q=P, u=2)
+            copy = nc.scalar.copy if i >= Q_TILES - 2 else nc.vector.tensor_copy
             for half in range(2):
-                nc.vector.tensor_copy(
+                copy(
                     out=words[:, 2 * half : 2 * half + 2, :, :],
                     in_=turned_of[i][half][:].rearrange("p g u q -> p g q u"),
                 )
@@ -426,9 +444,6 @@ def tile_hyperbolicattention_kernel(tc, query, keys, values, c, out):
                 accum_out=e_sum[:, i : i + 1],
             )
 
-        def invert_sum(i):
-            nc.vector.reciprocal(out=r_sum[:, i : i + 1], in_=e_sum[:, i : i + 1])
-
         for banks in BANK_HALVES:
             for bank in banks:
                 spread(kb_neg_row, kb_neg, bank * TURNS, psum_turn, "turn", nc.scalar.copy)
@@ -448,8 +463,8 @@ def tile_hyperbolicattention_kernel(tc, query, keys, values, c, out):
             nc.scalar.activation(out=r_pair[:, :, cols], in_=h_pair[:, :, cols], func=ACT.Sqrt)
 
         def add_roots(i):
-            for bank in range(0 if adds_on_vector(i) else BANKS_PER_ROW):
-                part = slice(bank * BANK, (bank + 1) * BANK)
+            for piece in range(0 if adds_on_vector(i) else ADD_PIECES):
+                part = slice(piece * NK // ADD_PIECES, (piece + 1) * NK // ADD_PIECES)
                 nc.gpsimd.tensor_add(
                     out=row_of[i][:, part], in0=row_of[i][:, part], in1=root_of[i][:, part]
                 )
@@ -480,21 +495,29 @@ def tile_hyperbolicattention_kernel(tc, query, keys, values, c, out):
             if cur and g > 0:
                 root_minima(cur)
                 for i in cur:
-                    if has_one_root(i):
+                    if has_one_root(i) and i not in root_of:
                         product_under_root(i)
                     square_roots(i)
                     add_roots(i)
 
+            if g > 0 and cur and not nxt:
+                minimum_terms(cur)
+            weighed = list(cur[:4] if g == 0 else cur[:3]) if nxt else []
+            points = 2 * len(nxt) - len(weighed)
+
+            def point(k):
+                if weighed and k >= points:
+                    normalise(weighed.pop(0))
+
             if old:
-                invert_sum(old[0])
-                normalise(old[0])
+                if old[0] not in weights_of:
+                    normalise(old[0])
                 turn_weights(old[0])
-            for j in range(max(len(old) + 1, len(nxt))):
-                if j + 1 < len(old):
-                    invert_sum(old[j + 1])
+            for j in range(max(len(old) + 1, len(nxt), 1)):
                 if j < len(nxt):
                     distance_terms(nxt[j])
-                if j + 1 < len(old):
+                point(2 * j)
+                if j + 1 < len(old) and old[j + 1] not in weights_of:
                     normalise(old[j + 1])
                 if j < len(old):
                     group_weights(old[j])
@@ -502,21 +525,27 @@ def tile_hyperbolicattention_kernel(tc, query, keys, values, c, out):
                     turn_weights(old[j + 1])
                 if j < len(nxt):
                     floor_and_min(nxt[j])
-                if j == 0 and cur and g > 0:
-                    minimum_terms(cur)
+                    if has_one_root(nxt[j]) and product_on_gpsimd(nxt[j]):
+                        product_under_root(nxt[j])
+                if j == 0 and cur:
+                    if g > 0 and nxt:
+                        minimum_terms(cur)
+                    for i in cur:
+                        if not adds_on_vector(i):
+                            logarithm(i)
                 for i in cur:
-                    if adds_on_vector(i) and j == i - 13:
+                    if adds_on_vector(i) and j == max(1, i - 13):
                         nc.vector.tensor_add(
                             out=row_of[i][:], in0=row_of[i][:], in1=root_of[i][:]
                         )
+                        logarithm(i)
+                if cur and j == (max([max(1, i - 13) for i in cur if adds_on_vector(i)], default=0)):
+                    for i in cur:
+                        exponential(i)
                 if j < len(old):
                     quantise_and_multiply(old[j])
                 if 0 <= j - 1 < len(old):
                     store(old[j - 1])
+                point(2 * j + 1)
             if nxt:
                 finish_minima(nxt)
-
-            for i in cur:
-                logarithm(i)
-            for i in cur:
-                exponential(i)

@@ -42,7 +42,7 @@ def tile_hyperbolicattention_kernel(tc, query, keys, values, c, out):
     with ExitStack() as ctx:
         ctx.enter_context(tc.manual_schedule())
         keep = ctx.enter_context(tc.tile_pool(name="keep", bufs=1))
-        rows = ctx.enter_context(tc.tile_pool(name="rows", bufs=19))
+        rows = ctx.enter_context(tc.tile_pool(name="rows", bufs=18))
         tail = ctx.enter_context(tc.tile_pool(name="tail", bufs=2))
         psum_scores = ctx.enter_context(tc.psum_pool(name="psum_scores", bufs=BANKS_PER_ROW))
         psum_turn = ctx.enter_context(tc.psum_pool(name="psum_turn", bufs=2))
@@ -62,7 +62,8 @@ def tile_hyperbolicattention_kernel(tc, query, keys, values, c, out):
             nc.sync.dma_start(out=nat[:, tiles, :], in_=view[:, tiles, :])
         v_raw = rows.tile([P, PASSES, PACK, DV], BF16, name="v_raw", tag="row", align_bytes=64)
         nc.sync.dma_start(
-            out=v_raw[:], in_=values.rearrange("(g p j) w -> p g j w", g=PASSES, p=P, j=PACK)
+            out=v_raw[:].rearrange("p g (u e) w -> p (g u) (e w)", u=2),
+            in_=values.rearrange("(h p e) w -> p h (e w)", p=P, e=2),
         )
 
         ident_bf = keep.tile([P, P], BF16, name="ident_bf")
@@ -140,6 +141,35 @@ def tile_hyperbolicattention_kernel(tc, query, keys, values, c, out):
         m_neg = keep.tile([P, Q_TILES], F32, name="m_neg")
         h_floor = keep.tile([P, Q_TILES], F32, name="h_floor")
 
+        k_feats = rows.tile([P, 2 * CHUNK, P], BF16, name="k_feats", tag="row", align_bytes=64)
+        q_feats = rows.tile([P, Q_TILES, P], BF16, name="q_feats", tag="row", align_bytes=64)
+        kT_norm = keep.tile([P, NK // 2], BF16, name="kT_norm")
+        qT_norm = keep.tile([P, NQ], BF16, name="qT_norm")
+        rest = keep.tile([P, Q_TILES], F32, name="rest")
+        nc.gpsimd.memset(k_feats[:], 0.0)
+        nc.gpsimd.memset(q_feats[:], 0.0)
+        nc.gpsimd.memset(k_feats[:, :, 3:6], 1.0)
+        nc.gpsimd.memset(q_feats[:, :, 0:3], 1.0)
+
+        def split_norms(feats, base, norms, tiles):
+            piece = [feats[:, tiles, base + n] for n in range(3)]
+            nc.gpsimd.tensor_scalar(
+                out=rest[:, tiles], in0=norms[:, tiles], scalar1=-0.5, scalar2=0.0,
+                op0=ALU.mult, op1=ALU.add,
+            )
+            nc.gpsimd.tensor_copy(out=piece[0], in_=rest[:, tiles])
+            nc.gpsimd.tensor_sub(out=rest[:, tiles], in0=rest[:, tiles], in1=piece[0])
+            nc.gpsimd.tensor_copy(out=piece[1], in_=rest[:, tiles])
+            nc.gpsimd.tensor_sub(out=piece[2], in0=rest[:, tiles], in1=piece[1])
+
+        def turn_norms(feats, t0, pool, tag, copy, dst):
+            turned = pool.tile([P, TURNS, P], BF16, name="turned_norm", tag=tag)
+            for r in range(TURNS):
+                nc.tensor.transpose(turned[:, r, :], feats[:, t0 + r, :], ident_bf[:])
+            copy(
+                out=dst[:, t0 * P : (t0 + TURNS) * P], in_=turned[:].rearrange("p r m -> p (r m)")
+            )
+
         def query_norms(t0):
             for t in range(t0, t0 + CHUNK):
                 nc.scalar.activation(
@@ -147,19 +177,18 @@ def tile_hyperbolicattention_kernel(tc, query, keys, values, c, out):
                     accum_out=uu[:, t : t + 1],
                 )
 
-        def query_terms(tiles):
-            nc.vector.tensor_scalar(
-                out=uu_term[:, tiles], in0=uu[:, tiles], scalar1=-0.5, scalar2=None, op0=ALU.mult
-            )
-            one_minus_clipped(a_q[:, tiles], uu[:, tiles])
-            nc.vector.tensor_scalar(
-                out=m_neg[:, tiles], in0=a_q[:, tiles], scalar1=kappa[:, 0:1], scalar2=-2.0 / EPS,
-                op0=ALU.mult, op1=ALU.mult,
-            )
-            nc.vector.tensor_scalar(
-                out=h_floor[:, tiles], in0=a_q[:, tiles], scalar1=EPS / 2.0, scalar2=None,
-                op0=ALU.mult,
-            )
+        def query_terms(engine, tiles):
+            for out, source, factor, op1, second in (
+                (uu_term, uu, -0.5, ALU.add, 0.0),
+                (a_q, uu, kappa[:, 0:1], ALU.min, 1.0 - EPS),
+                (a_q, a_q, -1.0, ALU.add, 1.0),
+                (m_neg, a_q, kappa[:, 0:1], ALU.mult, -2.0 / EPS),
+                (h_floor, a_q, EPS / 2.0, ALU.add, 0.0),
+            ):
+                engine.tensor_scalar(
+                    out=out[:, tiles], in0=source[:, tiles], scalar1=factor, scalar2=second,
+                    op0=ALU.mult, op1=op1,
+                )
 
         def turn_queries(t0):
             features = psum_out.tile([P, D_HALVES, TURNS, P], BF16, name="turned_q", tag="product")
@@ -168,6 +197,9 @@ def tile_hyperbolicattention_kernel(tc, query, keys, values, c, out):
                     nc.tensor.transpose(
                         features[:, h, r, :], q_nat[:, t0 + r, h * P : (h + 1) * P], ident_bf[:]
                     )
+            feats = psum_turn.tile([P, TURNS, P], BF16, name="turned_norm", tag="turn")
+            for r in range(TURNS):
+                nc.tensor.transpose(feats[:, r, :], q_feats[:, t0 + r, :], ident_bf[:])
             norms = psum_out.tile([P, TURNS, P], F32, name="turned_uu", tag="product")
             for r in range(TURNS):
                 nc.tensor.transpose(
@@ -180,6 +212,9 @@ def tile_hyperbolicattention_kernel(tc, query, keys, values, c, out):
                     nc.vector.tensor_copy(
                         out=qT[:, h, queries], in_=features[:, h, :, :].rearrange("p r m -> p (r m)")
                     )
+                nc.vector.tensor_copy(
+                    out=qT_norm[:, queries], in_=feats[:].rearrange("p r m -> p (r m)")
+                )
                 nc.vector.tensor_copy(
                     out=uu_row[:, queries], in_=norms[:].rearrange("p r m -> p (r m)")
                 )
@@ -196,7 +231,7 @@ def tile_hyperbolicattention_kernel(tc, query, keys, values, c, out):
                 out=key_squares[:, part, :, :], in_=k_nat[:, chunk, :], func=ACT.Square
             )
             turn_features(
-                k_nat, t0, psum_scores, "scores", (nc.vector.tensor_copy, nc.scalar.copy), kT
+                k_nat, t0, psum_scores, "scores", (nc.scalar.copy, nc.scalar.copy), kT
             )
             nc.vector.tensor_reduce(
                 out=run_sums[:],
@@ -221,7 +256,7 @@ def tile_hyperbolicattention_kernel(tc, query, keys, values, c, out):
 
         prepare_keys(0)
         query_norms(0)
-        query_terms(slice(0, CHUNK))
+        query_terms(nc.vector, slice(0, CHUNK))
         turn_features(
             q_nat, 0, psum_turn, "turn", (nc.vector.tensor_copy, nc.vector.tensor_copy), qT
         )
@@ -231,6 +266,8 @@ def tile_hyperbolicattention_kernel(tc, query, keys, values, c, out):
         prepare_keys(2 * CHUNK)
         prepare_keys(3 * CHUNK)
         key_factors(slice(2 * CHUNK, K_TILES))
+        split_norms(k_feats, 0, vv, slice(0, 2 * CHUNK))
+        split_norms(q_feats, 3, uu, slice(0, CHUNK))
 
         h_pair = keep.tile([P, 2, Q_TILES], F32, name="h_pair")
         r_pair = keep.tile([P, 2, Q_TILES], F32, name="r_pair")
@@ -248,6 +285,9 @@ def tile_hyperbolicattention_kernel(tc, query, keys, values, c, out):
         grouped_of = {}
         product_of = {}
 
+        def sums_norms(i, banks):
+            return banks[0] == 0 and 1 <= i < 13
+
         def scores(i, banks):
             queries = slice(i * P, (i + 1) * P)
             for bank in banks:
@@ -257,7 +297,13 @@ def tile_hyperbolicattention_kernel(tc, query, keys, values, c, out):
                     ps[:], lhsT=qT[:, 0, queries], rhs=kT[:, 0, bank * BANK : (bank + 1) * BANK],
                     start=True, stop=False,
                 )
-            for bank in banks:
+            if sums_norms(i, banks):
+                for bank in banks:
+                    nc.tensor.matmul(
+                        score_bank[(i, bank)][:], lhsT=qT_norm[:, queries],
+                        rhs=kT_norm[:, bank * BANK : (bank + 1) * BANK], start=False, stop=False,
+                    )
+            for bank in () if sums_norms(i, banks) else banks:
                 for r in range(TURNS):
                     for term in (rep_vv[:, bank * TURNS + r, :], uu_row[:, queries]):
                         nc.tensor.matmul(
@@ -296,7 +342,7 @@ def tile_hyperbolicattention_kernel(tc, query, keys, values, c, out):
             return i in (5, 6)
 
         def adds_on_vector(i):
-            return i >= 13
+            return i >= 10
 
         def product_under_root(i):
             root = rows.tile([P, NK], F32, name="root", tag="row", align_bytes=64)
@@ -331,7 +377,7 @@ def tile_hyperbolicattention_kernel(tc, query, keys, values, c, out):
         def normalise(i):
             weights = tail.tile([P, NK], BF16, name="weights", tag="weights", bufs=4)
             weights_of[i] = weights
-            engine = nc.gpsimd if i in (0, 1, 2, 3, 5, 6, 7, 12, 14) else nc.vector
+            engine = nc.gpsimd if i in (0, 1, 2, 3, 5, 6, 7) else nc.vector
             nc.vector.reciprocal(out=r_sum[:, i : i + 1], in_=e_sum[:, i : i + 1])
             engine.tensor_scalar(
                 out=weights[:], in0=row_of[i][:], scalar1=r_sum[:, i : i + 1], scalar2=0.0,
@@ -340,7 +386,7 @@ def tile_hyperbolicattention_kernel(tc, query, keys, values, c, out):
 
         def turn_weights(i):
             words = weights_of[i][:].bitcast(F32).rearrange(
-                "p (g m u) -> p g u m", g=PASSES, m=P, u=2
+                "p (g u m) -> p g u m", g=PASSES, m=P, u=2
             )
             turned_of[i] = []
             for half in range(2):
@@ -448,6 +494,9 @@ def tile_hyperbolicattention_kernel(tc, query, keys, values, c, out):
             for bank in banks:
                 spread(kb_neg_row, kb_neg, bank * TURNS, psum_turn, "turn", nc.scalar.copy)
             scores(0, banks)
+        for t0 in (0, CHUNK):
+            turn_norms(k_feats, t0, psum_turn, "turn", nc.scalar.copy, kT_norm)
+        turn_norms(q_feats, 0, psum_turn, "turn", nc.scalar.copy, qT_norm)
         for t0 in range(CHUNK, Q_TILES, CHUNK):
             query_norms(t0)
 
@@ -457,6 +506,9 @@ def tile_hyperbolicattention_kernel(tc, query, keys, values, c, out):
                 out=v_grouped[:, g, :, :], in0=v_raw[:, g, :, :].rearrange("p j w -> p w j"),
                 scalar1=1.0, scalar2=0.0, op0=ALU.mult, op1=ALU.add,
             )
+
+        query_terms(nc.gpsimd, slice(CHUNK, Q_TILES))
+        split_norms(q_feats, 3, uu, slice(CHUNK, Q_TILES))
 
         def root_minima(group):
             cols = slice(group[0], group[-1] + 1)
@@ -470,8 +522,6 @@ def tile_hyperbolicattention_kernel(tc, query, keys, values, c, out):
                 )
 
         for i in groups[0]:
-            if i == 1:
-                query_terms(slice(CHUNK, Q_TILES))
             distance_terms(i)
             floor_and_min(i)
             if i == groups[0][-1]:

@@ -49,7 +49,10 @@ def tile_hyperbolicattention_kernel(tc, query, keys, values, c, out):
         psum_out = ctx.enter_context(tc.psum_pool(name="psum_out", bufs=2))
 
         c_bf = keep.tile([P, 1], BF16, name="c_bf")
-        nc.sync.dma_start(out=c_bf[:], in_=c.partition_broadcast(P))
+        nc.vector.memset(c_bf[:], 0.0)
+        nc.scalar.dma_start(out=c_bf[0:1, :], in_=c.rearrange("(o n) -> o n", o=1))
+        ones_bf = keep.tile([P, 1], BF16, name="ones_bf")
+        nc.vector.memset(ones_bf[:], 1.0)
         k_nat = rows.tile([P, K_TILES, D], BF16, name="k_nat", tag="row", align_bytes=64)
         q_nat = rows.tile([P, Q_TILES, D], BF16, name="q_nat", tag="row", align_bytes=64)
         k_view = keys.rearrange("(t p) d -> p t d", p=P)
@@ -75,25 +78,6 @@ def tile_hyperbolicattention_kernel(tc, query, keys, values, c, out):
         nc.vector.memset(one[:], 1.0)
         warm = keep.tile([P, 1], F32, name="warm")
         nc.scalar.activation(out=warm[:], in_=one[:], func=ACT.Sqrt)
-
-        kappa = keep.tile([P, 1], F32, name="kappa")
-        nc.scalar.activation(out=kappa[:], in_=c_bf[:], func=ACT.Abs)
-        nc.vector.tensor_scalar(
-            out=kappa[:], in0=kappa[:], scalar1=EPS, scalar2=EPS, op0=ALU.add, op1=ALU.max
-        )
-        nc.vector.tensor_scalar(
-            out=kappa[:], in0=kappa[:], scalar1=1.0 - EPS, scalar2=None, op0=ALU.min
-        )
-        neg_p = keep.tile([P, 1], F32, name="neg_p")
-        nc.scalar.activation(out=neg_p[:], in_=kappa[:], func=ACT.Sqrt)
-        nc.vector.reciprocal(out=neg_p[:], in_=neg_p[:])
-        nc.vector.tensor_scalar(
-            out=neg_p[:], in0=neg_p[:], scalar1=-2.0, scalar2=None, op0=ALU.mult
-        )
-        neg_half_p = keep.tile([P, 1], F32, name="neg_half_p")
-        nc.vector.tensor_scalar(
-            out=neg_half_p[:], in0=neg_p[:], scalar1=0.5, scalar2=None, op0=ALU.mult
-        )
 
         vv = keep.tile([P, K_TILES], F32, name="vv")
         uu = keep.tile([P, Q_TILES], F32, name="uu")
@@ -177,9 +161,14 @@ def tile_hyperbolicattention_kernel(tc, query, keys, values, c, out):
                     accum_out=uu[:, t : t + 1],
                 )
 
+        def half_norms(engine, tiles):
+            engine.tensor_scalar(
+                out=uu_term[:, tiles], in0=uu[:, tiles], scalar1=-0.5, scalar2=0.0,
+                op0=ALU.mult, op1=ALU.add,
+            )
+
         def query_terms(engine, tiles):
             for out, source, factor, op1, second in (
-                (uu_term, uu, -0.5, ALU.add, 0.0),
                 (a_q, uu, kappa[:, 0:1], ALU.min, 1.0 - EPS),
                 (a_q, a_q, -1.0, ALU.add, 1.0),
                 (m_neg, a_q, kappa[:, 0:1], ALU.mult, -2.0 / EPS),
@@ -208,14 +197,15 @@ def tile_hyperbolicattention_kernel(tc, query, keys, values, c, out):
 
             def take():
                 queries = slice(t0 * P, (t0 + TURNS) * P)
+                copy = nc.scalar.copy if t0 == CHUNK else nc.vector.tensor_copy
                 for h in range(D_HALVES):
-                    nc.vector.tensor_copy(
+                    copy(
                         out=qT[:, h, queries], in_=features[:, h, :, :].rearrange("p r m -> p (r m)")
                     )
-                nc.vector.tensor_copy(
+                copy(
                     out=qT_norm[:, queries], in_=feats[:].rearrange("p r m -> p (r m)")
                 )
-                nc.vector.tensor_copy(
+                copy(
                     out=uu_row[:, queries], in_=norms[:].rearrange("p r m -> p (r m)")
                 )
 
@@ -256,18 +246,33 @@ def tile_hyperbolicattention_kernel(tc, query, keys, values, c, out):
 
         prepare_keys(0)
         query_norms(0)
-        query_terms(nc.vector, slice(0, CHUNK))
+        half_norms(nc.vector, slice(0, CHUNK))
         turn_features(
             q_nat, 0, psum_turn, "turn", (nc.vector.tensor_copy, nc.vector.tensor_copy), qT
         )
         prepare_keys(CHUNK)
         spread(uu_row, uu_term, 0, psum_turn, "turn", nc.vector.tensor_copy)
+        c_all = psum_out.tile([P, 1], F32, name="c_all", tag="product")
+        nc.tensor.matmul(
+            c_all[:], lhsT=c_bf[:].to_broadcast([P, P]), rhs=ones_bf[:], start=True, stop=True
+        )
+        kappa = keep.tile([P, 1], F32, name="kappa")
+        nc.scalar.activation(out=kappa[:], in_=c_all[:], func=ACT.Abs)
+        nc.vector.tensor_scalar(
+            out=kappa[:], in0=kappa[:], scalar1=EPS, scalar2=EPS, op0=ALU.add, op1=ALU.max
+        )
+        nc.vector.tensor_scalar(
+            out=kappa[:], in0=kappa[:], scalar1=1.0 - EPS, scalar2=None, op0=ALU.min
+        )
         key_factors(slice(0, 2 * CHUNK))
+        query_terms(nc.vector, slice(0, CHUNK))
+        split_norms(k_feats, 0, vv, slice(0, 2 * CHUNK))
+        split_norms(q_feats, 3, uu, slice(0, CHUNK))
         prepare_keys(2 * CHUNK)
         prepare_keys(3 * CHUNK)
         key_factors(slice(2 * CHUNK, K_TILES))
-        split_norms(k_feats, 0, vv, slice(0, 2 * CHUNK))
-        split_norms(q_feats, 3, uu, slice(0, CHUNK))
+        neg_p = keep.tile([P, 1], F32, name="neg_p")
+        nc.scalar.activation(out=neg_p[:], in_=kappa[:], func=ACT.Sqrt)
 
         h_pair = keep.tile([P, 2, Q_TILES], F32, name="h_pair")
         r_pair = keep.tile([P, 2, Q_TILES], F32, name="r_pair")
@@ -283,6 +288,8 @@ def tile_hyperbolicattention_kernel(tc, query, keys, values, c, out):
         weights_of = {}
         turned_of = {}
         grouped_of = {}
+        codes_of = {}
+        scales_of = {}
         product_of = {}
 
         def sums_norms(i, banks):
@@ -374,52 +381,64 @@ def tile_hyperbolicattention_kernel(tc, query, keys, values, c, out):
                 out=row_of[i][:], in_=row_of[i][:], func=ACT.Sqrt, bias=a_q[:, i : i + 1]
             )
 
-        def normalise(i):
-            weights = tail.tile([P, NK], BF16, name="weights", tag="weights", bufs=4)
-            weights_of[i] = weights
+        def normalise(i, halves=(0, 1)):
+            if halves[0] == 0:
+                weights_of[i] = tail.tile([P, NK], BF16, name="weights", tag="weights", bufs=4)
+                nc.vector.reciprocal(out=r_sum[:, i : i + 1], in_=e_sum[:, i : i + 1])
             engine = nc.gpsimd if i in (0, 1, 2, 3, 5, 6, 7) else nc.vector
-            nc.vector.reciprocal(out=r_sum[:, i : i + 1], in_=e_sum[:, i : i + 1])
+            cols = slice(halves[0] * NK // 2, (halves[-1] + 1) * NK // 2)
             engine.tensor_scalar(
-                out=weights[:], in0=row_of[i][:], scalar1=r_sum[:, i : i + 1], scalar2=0.0,
-                op0=ALU.mult, op1=ALU.add,
+                out=weights_of[i][:, cols], in0=row_of[i][:, cols], scalar1=r_sum[:, i : i + 1],
+                scalar2=0.0, op0=ALU.mult, op1=ALU.add,
             )
 
-        def turn_weights(i):
+        def turn_weights(i, halves=(0, 1)):
             words = weights_of[i][:].bitcast(F32).rearrange(
                 "p (g u m) -> p g u m", g=PASSES, m=P, u=2
             )
-            turned_of[i] = []
-            for half in range(2):
+            for half in halves:
                 turned = psum_turn.tile([P, 2, 2, P], F32, name="turned_w", tag="turn")
                 for g in range(2):
                     for u in range(2):
                         nc.tensor.transpose(
                             turned[:, g, u, :], words[:, 2 * half + g, u, :], ident_f32[:]
                         )
-                turned_of[i].append(turned)
+                turned_of[(i, half)] = turned
 
-        def group_weights(i):
-            grouped = tail.tile([P, NK], BF16, name="grouped", tag="grouped", align_bytes=64)
-            grouped_of[i] = grouped
-            words = grouped[:].bitcast(F32).rearrange("p (g q u) -> p g q u", g=PASSES, q=P, u=2)
+        def group_weights(i, halves=(0, 1)):
+            if halves[0] == 0:
+                grouped_of[i] = tail.tile(
+                    [P, NK], BF16, name="grouped", tag="grouped", align_bytes=64
+                )
+            words = grouped_of[i][:].bitcast(F32).rearrange(
+                "p (g q u) -> p g q u", g=PASSES, q=P, u=2
+            )
             copy = nc.scalar.copy if i >= Q_TILES - 2 else nc.vector.tensor_copy
-            for half in range(2):
+            for half in halves:
                 copy(
                     out=words[:, 2 * half : 2 * half + 2, :, :],
-                    in_=turned_of[i][half][:].rearrange("p g u q -> p g q u"),
+                    in_=turned_of[(i, half)][:].rearrange("p g u q -> p g q u"),
                 )
 
-        def quantise_and_multiply(i):
-            codes = tail.tile([P, PASSES * P], U32, name="codes", tag="codes", align_bytes=64)
-            scales = tail.tile([P, PASSES * P], U8, name="scales", tag="scales", align_bytes=64)
+        def quantise_and_multiply(i, halves=(0, 1)):
+            if halves[0] == 0:
+                codes_of[i] = tail.tile(
+                    [P, PASSES * P], U32, name="codes", tag="codes", align_bytes=64
+                )
+                scales_of[i] = tail.tile(
+                    [P, PASSES * P], U8, name="scales", tag="scales", align_bytes=64
+                )
+                product_of[i] = psum_out.tile([P, DV], F32, name="product", tag="product")
+            codes, scales = codes_of[i], scales_of[i]
+            passes = range(halves[0] * PASSES // 2, (halves[-1] + 1) * PASSES // 2)
+            words = slice(passes[0] * P, (passes[-1] + 1) * P)
             nc.vector.quantize_mx(
-                out=codes[:].bitcast(FP8X4), scales=scales[:], in_=grouped_of[i][:]
+                out=codes[:, words].bitcast(FP8X4), scales=scales[:, words],
+                in_=grouped_of[i][:, passes[0] * P * PACK : (passes[-1] + 1) * P * PACK],
             )
-            product = psum_out.tile([P, DV], F32, name="product", tag="product")
-            product_of[i] = product
-            for g in range(PASSES):
+            for g in passes:
                 nc.tensor.matmul_mx(
-                    out=product[:],
+                    out=product_of[i][:],
                     lhsT=codes[:, g * P : (g + 1) * P].bitcast(FP8X4),
                     lhsT_scale=scales[:, g * P : (g + 1) * P],
                     rhs=v_codes[:, g * DV : (g + 1) * DV].bitcast(FP8X4),
@@ -494,11 +513,11 @@ def tile_hyperbolicattention_kernel(tc, query, keys, values, c, out):
             for bank in banks:
                 spread(kb_neg_row, kb_neg, bank * TURNS, psum_turn, "turn", nc.scalar.copy)
             scores(0, banks)
+        query_norms(CHUNK)
+        query_norms(2 * CHUNK)
         for t0 in (0, CHUNK):
             turn_norms(k_feats, t0, psum_turn, "turn", nc.scalar.copy, kT_norm)
         turn_norms(q_feats, 0, psum_turn, "turn", nc.scalar.copy, qT_norm)
-        for t0 in range(CHUNK, Q_TILES, CHUNK):
-            query_norms(t0)
 
         v_grouped = rows.tile([P, PASSES, DV, PACK], BF16, name="v_grouped", tag="row", align_bytes=64)
         for g in range(PASSES):
@@ -507,8 +526,12 @@ def tile_hyperbolicattention_kernel(tc, query, keys, values, c, out):
                 scalar1=1.0, scalar2=0.0, op0=ALU.mult, op1=ALU.add,
             )
 
-        query_terms(nc.gpsimd, slice(CHUNK, Q_TILES))
-        split_norms(q_feats, 3, uu, slice(CHUNK, Q_TILES))
+        def later_terms(tiles):
+            half_norms(nc.gpsimd, tiles)
+            query_terms(nc.gpsimd, tiles)
+            split_norms(q_feats, 3, uu, tiles)
+
+        later_terms(slice(CHUNK, 3 * CHUNK))
 
         def root_minima(group):
             cols = slice(group[0], group[-1] + 1)
@@ -528,8 +551,20 @@ def tile_hyperbolicattention_kernel(tc, query, keys, values, c, out):
                 finish_minima(groups[0])
                 root_minima(groups[0])
             square_roots(i)
+            if i == 0:
+                query_norms(3 * CHUNK)
             add_roots(i)
+            if i == 0:
+                later_terms(slice(3 * CHUNK, Q_TILES))
 
+        nc.vector.reciprocal(out=neg_p[:], in_=neg_p[:])
+        nc.vector.tensor_scalar(
+            out=neg_p[:], in0=neg_p[:], scalar1=-2.0, scalar2=None, op0=ALU.mult
+        )
+        neg_half_p = keep.tile([P, 1], F32, name="neg_half_p")
+        nc.vector.tensor_scalar(
+            out=neg_half_p[:], in0=neg_p[:], scalar1=0.5, scalar2=None, op0=ALU.mult
+        )
         v_codes = keep.tile([P, PASSES * DV], U32, name="v_codes", align_bytes=64)
         v_scales = keep.tile([P, PASSES * DV], U8, name="v_scales", align_bytes=64)
         nc.vector.quantize_mx(
@@ -567,8 +602,11 @@ def tile_hyperbolicattention_kernel(tc, query, keys, values, c, out):
                 if j < len(nxt):
                     distance_terms(nxt[j])
                 point(2 * j)
+                split = not cur and j == len(old) - 2
                 if j + 1 < len(old) and old[j + 1] not in weights_of:
-                    normalise(old[j + 1])
+                    normalise(old[j + 1], (0,) if split else (0, 1))
+                    if split:
+                        normalise(old[j + 1], (1,))
                 if j < len(old):
                     group_weights(old[j])
                 if j + 1 < len(old):
@@ -592,7 +630,10 @@ def tile_hyperbolicattention_kernel(tc, query, keys, values, c, out):
                 if cur and j == (max([max(1, i - 13) for i in cur if adds_on_vector(i)], default=0)):
                     for i in cur:
                         exponential(i)
-                if j < len(old):
+                if j < len(old) and not cur and j == len(old) - 1:
+                    quantise_and_multiply(old[j], (0,))
+                    quantise_and_multiply(old[j], (1,))
+                elif j < len(old):
                     quantise_and_multiply(old[j])
                 if 0 <= j - 1 < len(old):
                     store(old[j - 1])

from contextlib import ExitStack

import concourse.mybir as mybir
from concourse.masks import make_identity

F32 = mybir.dt.float32
BF16 = mybir.dt.bfloat16
U32 = mybir.dt.uint32
U8 = mybir.dt.uint8
FP8X4 = mybir.dt.float8_e4m3fn_x4
ALU = mybir.AluOpType
ACT = mybir.ActivationFunctionType

NQ, NK, D, DV = 2048, 2048, 256, 256
EPS = 1e-7
P = 128
Q_TILES = NQ // P
K_TILES = NK // P
D_HALVES = D // P
BANK = 512
BANKS_PER_ROW = NK // BANK
BANK_HALVES = ((0, 1), (2, 3))
TURNS = BANK // P
PACK = 4
K_PASS = P * PACK
PASSES = NK // K_PASS
CHUNK = 4
RUN = 16
GROUP_SIZES = (5, 5, 6)
ADD_PIECES = 2
JUNK_SLOTS = 8

assert CHUNK == TURNS
assert sum(GROUP_SIZES) == Q_TILES
assert D_HALVES == 2

FLOPS = 2 * NQ * NK * D + 2 * NQ * NK * DV


def tile_hyperbolicattention_kernel(tc, query, keys, values, c, out):
    nc = tc.nc
    with ExitStack() as ctx:
        ctx.enter_context(tc.manual_schedule())
        keep = ctx.enter_context(tc.tile_pool(name="keep", bufs=1))
        rows = ctx.enter_context(tc.tile_pool(name="rows", bufs=18))
        tail = ctx.enter_context(tc.tile_pool(name="tail", bufs=2))
        psum_scores = ctx.enter_context(tc.psum_pool(name="psum_scores", bufs=BANKS_PER_ROW))
        psum_turn = ctx.enter_context(tc.psum_pool(name="psum_turn", bufs=2))
        psum_out = ctx.enter_context(tc.psum_pool(name="psum_out", bufs=2))

        c_bf = keep.tile([P, 1], BF16, name="c_bf")
        nc.vector.memset(c_bf[:], 0.0)
        nc.scalar.dma_start(out=c_bf[0:1, :], in_=c.rearrange("(o n) -> o n", o=1))
        ones_bf = keep.tile([P, 1], BF16, name="ones_bf")
        nc.vector.memset(ones_bf[:], 1.0)
        k_nat = rows.tile([P, K_TILES, D], BF16, name="k_nat", tag="row", align_bytes=64)
        q_nat = rows.tile([P, Q_TILES, D], BF16, name="q_nat", tag="row", align_bytes=64)
        k_view = keys.rearrange("(t p) d -> p t d", p=P)
        q_view = query.rearrange("(t p) d -> p t d", p=P)
        for nat, view, chunk in (
            (k_nat, k_view, 0), (q_nat, q_view, 0), (k_nat, k_view, 1), (k_nat, k_view, 2),
            (k_nat, k_view, 3), (q_nat, q_view, 1), (q_nat, q_view, 2), (q_nat, q_view, 3),
        ):
            tiles = slice(chunk * CHUNK, (chunk + 1) * CHUNK)
            nc.sync.dma_start(out=nat[:, tiles, :], in_=view[:, tiles, :])
        v_raw = rows.tile([P, PASSES, PACK, DV], BF16, name="v_raw", tag="row", align_bytes=64)
        nc.sync.dma_start(
            out=v_raw[:].rearrange("p g (u e) w -> p (g u) (e w)", u=2),
            in_=values.rearrange("(h p e) w -> p h (e w)", p=P, e=2),
        )

        ident_bf = keep.tile([P, P], BF16, name="ident_bf")
        make_identity(nc, ident_bf[:])
        ident_f32 = keep.tile([P, P], F32, name="ident_f32")
        make_identity(nc, ident_f32[:])

        one = keep.tile([P, 1], F32, name="one")
        nc.vector.memset(one[:], 1.0)
        warm = keep.tile([P, 1], F32, name="warm")
        nc.scalar.activation(out=warm[:], in_=one[:], func=ACT.Sqrt)

        vv = keep.tile([P, K_TILES], F32, name="vv")
        uu = keep.tile([P, Q_TILES], F32, name="uu")
        kT = keep.tile([P, D_HALVES, NK], BF16, name="kT")
        qT = keep.tile([P, D_HALVES, NQ], BF16, name="qT")
        rep_vv = keep.tile([P, K_TILES, P], F32, name="rep_vv")
        kb_neg = keep.tile([P, K_TILES], F32, name="kb_neg")
        kb_neg_row = keep.tile([P, NK], F32, name="kb_neg_row")

        def turn_features(nat, t0, pool, tag, copies, dst):
            for h in range(D_HALVES):
                turned = pool.tile([P, TURNS, P], BF16, name="turned_bf", tag=tag)
                for r in range(TURNS):
                    nc.tensor.transpose(
                        turned[:, r, :], nat[:, t0 + r, h * P : (h + 1) * P], ident_bf[:]
                    )
                copies[h](
                    out=dst[:, h, t0 * P : (t0 + TURNS) * P],
                    in_=turned[:].rearrange("p r m -> p (r m)"),
                )

        def one_minus_clipped(dst, sq_norms):
            nc.vector.tensor_scalar(
                out=dst, in0=sq_norms, scalar1=kappa[:, 0:1], scalar2=1.0 - EPS,
                op0=ALU.mult, op1=ALU.min,
            )
            nc.vector.tensor_scalar(
                out=dst, in0=dst, scalar1=-1.0, scalar2=1.0, op0=ALU.mult, op1=ALU.add
            )

        def spread(row, per_row, t0, pool, tag, copy):
            turned = pool.tile([P, TURNS, P], F32, name="turned_col", tag=tag)
            for r in range(TURNS):
                nc.tensor.transpose(
                    turned[:, r, :], per_row[:, t0 + r : t0 + r + 1].to_broadcast([P, P]), ident_f32[:]
                )
            copy(
                out=row[:, t0 * P : (t0 + TURNS) * P], in_=turned[:].rearrange("p r m -> p (r m)")
            )

        squares = rows.tile([P, JUNK_SLOTS, D], BF16, name="squares", tag="row", align_bytes=64)
        uu_term = keep.tile([P, Q_TILES], F32, name="uu_term")
        uu_row = keep.tile([P, NQ], F32, name="uu_row")
        a_q = keep.tile([P, Q_TILES], F32, name="a_q")
        m_neg = keep.tile([P, Q_TILES], F32, name="m_neg")
        h_floor = keep.tile([P, Q_TILES], F32, name="h_floor")

        k_feats = rows.tile([P, 2 * CHUNK, P], BF16, name="k_feats", tag="row", align_bytes=64)
        q_feats = rows.tile([P, Q_TILES, P], BF16, name="q_feats", tag="row", align_bytes=64)
        kT_norm = keep.tile([P, NK // 2], BF16, name="kT_norm")
        qT_norm = keep.tile([P, NQ], BF16, name="qT_norm")
        rest = keep.tile([P, Q_TILES], F32, name="rest")
        nc.gpsimd.memset(k_feats[:], 0.0)
        nc.gpsimd.memset(q_feats[:], 0.0)
        nc.gpsimd.memset(k_feats[:, :, 3:6], 1.0)
        nc.gpsimd.memset(q_feats[:, :, 0:3], 1.0)

        def split_norms(feats, base, norms, tiles):
            piece = [feats[:, tiles, base + n] for n in range(3)]
            nc.gpsimd.tensor_scalar(
                out=rest[:, tiles], in0=norms[:, tiles], scalar1=-0.5, scalar2=0.0,
                op0=ALU.mult, op1=ALU.add,
            )
            nc.gpsimd.tensor_copy(out=piece[0], in_=rest[:, tiles])
            nc.gpsimd.tensor_sub(out=rest[:, tiles], in0=rest[:, tiles], in1=piece[0])
            nc.gpsimd.tensor_copy(out=piece[1], in_=rest[:, tiles])
            nc.gpsimd.tensor_sub(out=piece[2], in0=rest[:, tiles], in1=piece[1])

        def turn_norms(feats, t0, pool, tag, copy, dst):
            turned = pool.tile([P, TURNS, P], BF16, name="turned_norm", tag=tag)
            for r in range(TURNS):
                nc.tensor.transpose(turned[:, r, :], feats[:, t0 + r, :], ident_bf[:])
            copy(
                out=dst[:, t0 * P : (t0 + TURNS) * P], in_=turned[:].rearrange("p r m -> p (r m)")
            )

        def query_norms(t0):
            for t in range(t0, t0 + CHUNK):
                nc.scalar.activation(
                    out=squares[:, t % JUNK_SLOTS, :], in_=q_nat[:, t, :], func=ACT.Square,
                    accum_out=uu[:, t : t + 1],
                )

        def half_norms(engine, tiles):
            engine.tensor_scalar(
                out=uu_term[:, tiles], in0=uu[:, tiles], scalar1=-0.5, scalar2=0.0,
                op0=ALU.mult, op1=ALU.add,
            )

        def query_terms(engine, tiles):
            for out, source, factor, op1, second in (
                (a_q, uu, kappa[:, 0:1], ALU.min, 1.0 - EPS),
                (a_q, a_q, -1.0, ALU.add, 1.0),
                (m_neg, a_q, kappa[:, 0:1], ALU.mult, -2.0 / EPS),
                (h_floor, a_q, EPS / 2.0, ALU.add, 0.0),
            ):
                engine.tensor_scalar(
                    out=out[:, tiles], in0=source[:, tiles], scalar1=factor, scalar2=second,
                    op0=ALU.mult, op1=op1,
                )

        def turn_queries(t0):
            features = psum_out.tile([P, D_HALVES, TURNS, P], BF16, name="turned_q", tag="product")
            for h in range(D_HALVES):
                for r in range(TURNS):
                    nc.tensor.transpose(
                        features[:, h, r, :], q_nat[:, t0 + r, h * P : (h + 1) * P], ident_bf[:]
                    )
            feats = psum_turn.tile([P, TURNS, P], BF16, name="turned_norm", tag="turn")
            for r in range(TURNS):
                nc.tensor.transpose(feats[:, r, :], q_feats[:, t0 + r, :], ident_bf[:])
            norms = psum_out.tile([P, TURNS, P], F32, name="turned_uu", tag="product")
            for r in range(TURNS):
                nc.tensor.transpose(
                    norms[:, r, :], uu_term[:, t0 + r : t0 + r + 1].to_broadcast([P, P]), ident_f32[:]
                )

            def take():
                queries = slice(t0 * P, (t0 + TURNS) * P)
                copy = nc.scalar.copy if t0 == CHUNK else nc.vector.tensor_copy
                for h in range(D_HALVES):
                    copy(
                        out=qT[:, h, queries], in_=features[:, h, :, :].rearrange("p r m -> p (r m)")
                    )
                copy(
                    out=qT_norm[:, queries], in_=feats[:].rearrange("p r m -> p (r m)")
                )
                copy(
                    out=uu_row[:, queries], in_=norms[:].rearrange("p r m -> p (r m)")
                )

            return take

        key_squares = rows.tile([P, 2, CHUNK, D], F32, name="key_squares", tag="row", align_bytes=64)
        run_sums = keep.tile([P, CHUNK, D // RUN], F32, name="run_sums")

        def prepare_keys(t0):
            chunk = slice(t0, t0 + CHUNK)
            part = t0 // CHUNK % 2
            nc.scalar.activation(
                out=key_squares[:, part, :, :], in_=k_nat[:, chunk, :], func=ACT.Square
            )
            turn_features(
                k_nat, t0, psum_scores, "scores", (nc.scalar.copy, nc.scalar.copy), kT
            )
            nc.vector.tensor_reduce(
                out=run_sums[:],
                in_=key_squares[:, part, :, :].rearrange("p t (a b) -> p t a b", b=RUN),
                axis=mybir.AxisListType.X, op=ALU.add,
            )
            nc.vector.tensor_reduce(
                out=vv[:, chunk], in_=run_sums[:], axis=mybir.AxisListType.X, op=ALU.add
            )
            nc.gpsimd.tensor_scalar(
                out=rep_vv[:, chunk, :], in0=vv[:, chunk].unsqueeze(2).to_broadcast([P, CHUNK, P]),
                scalar1=-0.5, scalar2=0.0, op0=ALU.mult, op1=ALU.add,
            )

        def key_factors(tiles):
            one_minus_clipped(kb_neg[:, tiles], vv[:, tiles])
            nc.vector.reciprocal(out=kb_neg[:, tiles], in_=kb_neg[:, tiles])
            nc.vector.tensor_scalar(
                out=kb_neg[:, tiles], in0=kb_neg[:, tiles], scalar1=kappa[:, 0:1], scalar2=-2.0,
                op0=ALU.mult, op1=ALU.mult,
            )

        prepare_keys(0)
        query_norms(0)
        half_norms(nc.vector, slice(0, CHUNK))
        turn_features(
            q_nat, 0, psum_turn, "turn", (nc.vector.tensor_copy, nc.vector.tensor_copy), qT
        )
        prepare_keys(CHUNK)
        spread(uu_row, uu_term, 0, psum_turn, "turn", nc.vector.tensor_copy)
        c_all = psum_out.tile([P, 1], F32, name="c_all", tag="product")
        nc.tensor.matmul(
            c_all[:], lhsT=c_bf[:].to_broadcast([P, P]), rhs=ones_bf[:], start=True, stop=True
        )
        kappa = keep.tile([P, 1], F32, name="kappa")
        nc.scalar.activation(out=kappa[:], in_=c_all[:], func=ACT.Abs)
        nc.vector.tensor_scalar(
            out=kappa[:], in0=kappa[:], scalar1=EPS, scalar2=EPS, op0=ALU.add, op1=ALU.max
        )
        nc.vector.tensor_scalar(
            out=kappa[:], in0=kappa[:], scalar1=1.0 - EPS, scalar2=None, op0=ALU.min
        )
        key_factors(slice(0, 2 * CHUNK))
        query_terms(nc.vector, slice(0, CHUNK))
        split_norms(k_feats, 0, vv, slice(0, 2 * CHUNK))
        split_norms(q_feats, 3, uu, slice(0, CHUNK))
        prepare_keys(2 * CHUNK)
        prepare_keys(3 * CHUNK)
        key_factors(slice(2 * CHUNK, K_TILES))
        neg_p = keep.tile([P, 1], F32, name="neg_p")
        nc.scalar.activation(out=neg_p[:], in_=kappa[:], func=ACT.Sqrt)

        h_pair = keep.tile([P, 2, Q_TILES], F32, name="h_pair")
        r_pair = keep.tile([P, 2, Q_TILES], F32, name="r_pair")
        inv_s_min = keep.tile([P, Q_TILES], F32, name="inv_s_min")
        inv_s_min_sq = keep.tile([P, Q_TILES], F32, name="inv_s_min_sq")
        shift = keep.tile([P, Q_TILES], F32, name="shift")
        e_sum = keep.tile([P, Q_TILES], F32, name="e_sum")
        r_sum = keep.tile([P, Q_TILES], F32, name="r_sum")

        score_bank = {}
        row_of = {}
        root_of = {}
        weights_of = {}
        turned_of = {}
        grouped_of = {}
        codes_of = {}
        scales_of = {}
        product_of = {}

        def sums_norms(i, banks):
            return banks[0] == 0 and 1 <= i < 13

        def scores(i, banks):
            queries = slice(i * P, (i + 1) * P)
            for bank in banks:
                ps = psum_scores.tile([P, BANK], F32, name="ps", tag="scores")
                score_bank[(i, bank)] = ps
                nc.tensor.matmul(
                    ps[:], lhsT=qT[:, 0, queries], rhs=kT[:, 0, bank * BANK : (bank + 1) * BANK],
                    start=True, stop=False,
                )
            if sums_norms(i, banks):
                for bank in banks:
                    nc.tensor.matmul(
                        score_bank[(i, bank)][:], lhsT=qT_norm[:, queries],
                        rhs=kT_norm[:, bank * BANK : (bank + 1) * BANK], start=False, stop=False,
                    )
            for bank in () if sums_norms(i, banks) else banks:
                for r in range(TURNS):
                    for term in (rep_vv[:, bank * TURNS + r, :], uu_row[:, queries]):
                        nc.tensor.matmul(
                            score_bank[(i, bank)][:, r * P : (r + 1) * P], lhsT=term,
                            rhs=ident_f32[:], is_transpose=True, start=False, stop=False,
                        )
            for bank in banks:
                nc.tensor.matmul(
                    score_bank[(i, bank)][:], lhsT=qT[:, 1, queries],
                    rhs=kT[:, 1, bank * BANK : (bank + 1) * BANK], start=False, stop=True,
                )

        def scaled_differences(i):
            row = rows.tile([P, NK], F32, name="row", tag="row", align_bytes=64)
            row_of[i] = row
            for banks in BANK_HALVES:
                for bank in banks:
                    cols = slice(bank * BANK, (bank + 1) * BANK)
                    nc.vector.scalar_tensor_tensor(
                        out=row[:, cols], in0=kb_neg_row[:, cols], scalar=m_neg[:, i : i + 1],
                        in1=score_bank[(i, bank)][:], op0=ALU.max, op1=ALU.mult,
                    )
                if i + 1 < Q_TILES:
                    scores(i + 1, banks)

        def floor_and_min(i):
            nc.vector.tensor_scalar(
                out=row_of[i][:], in0=row_of[i][:], scalar1=h_floor[:, i : i + 1], scalar2=None,
                op0=ALU.max, op1=ALU.min, accum_out=h_pair[:, 0, i : i + 1],
            )

        def has_one_root(i):
            return i in (5, 6) or i >= 12

        def product_on_gpsimd(i):
            return i in (5, 6)

        def adds_on_vector(i):
            return i >= 10

        def product_under_root(i):
            root = rows.tile([P, NK], F32, name="root", tag="row", align_bytes=64)
            root_of[i] = root
            if product_on_gpsimd(i):
                for piece in range(1):
                    part = slice(piece * NK // 1, (piece + 1) * NK // 1)
                    nc.gpsimd.tensor_scalar(
                        out=root[:, part], in0=row_of[i][:, part], scalar1=a_q[:, i : i + 1],
                        scalar2=1.0, op0=ALU.add, op1=ALU.mult,
                    )
                    nc.gpsimd.tensor_mul(
                        out=root[:, part], in0=root[:, part], in1=row_of[i][:, part]
                    )
            else:
                nc.vector.scalar_tensor_tensor(
                    out=root[:], in0=row_of[i][:], scalar=a_q[:, i : i + 1], in1=row_of[i][:],
                    op0=ALU.add, op1=ALU.mult,
                )

        def square_roots(i):
            if has_one_root(i):
                nc.scalar.activation(out=root_of[i][:], in_=root_of[i][:], func=ACT.Sqrt)
                return
            root = rows.tile([P, NK], F32, name="root", tag="row", align_bytes=64)
            root_of[i] = root
            nc.scalar.activation(out=root[:], in_=row_of[i][:], func=ACT.Sqrt)
            nc.scalar.activation(
                out=row_of[i][:], in_=row_of[i][:], func=ACT.Sqrt, bias=a_q[:, i : i + 1]
            )

        def normalise(i, halves=(0, 1)):
            if halves[0] == 0:
                weights_of[i] = tail.tile([P, NK], BF16, name="weights", tag="weights", bufs=4)
                nc.vector.reciprocal(out=r_sum[:, i : i + 1], in_=e_sum[:, i : i + 1])
            engine = nc.gpsimd if i in (0, 1, 2, 3, 5, 6, 7) else nc.vector
            cols = slice(halves[0] * NK // 2, (halves[-1] + 1) * NK // 2)
            engine.tensor_scalar(
                out=weights_of[i][:, cols], in0=row_of[i][:, cols], scalar1=r_sum[:, i : i + 1],
                scalar2=0.0, op0=ALU.mult, op1=ALU.add,
            )

        def turn_weights(i, halves=(0, 1)):
            words = weights_of[i][:].bitcast(F32).rearrange(
                "p (g u m) -> p g u m", g=PASSES, m=P, u=2
            )
            for half in halves:
                turned = psum_turn.tile([P, 2, 2, P], F32, name="turned_w", tag="turn")
                for g in range(2):
                    for u in range(2):
                        nc.tensor.transpose(
                            turned[:, g, u, :], words[:, 2 * half + g, u, :], ident_f32[:]
                        )
                turned_of[(i, half)] = turned

        def group_weights(i, halves=(0, 1)):
            if halves[0] == 0:
                grouped_of[i] = tail.tile(
                    [P, NK], BF16, name="grouped", tag="grouped", align_bytes=64
                )
            words = grouped_of[i][:].bitcast(F32).rearrange(
                "p (g q u) -> p g q u", g=PASSES, q=P, u=2
            )
            copy = nc.scalar.copy if i >= Q_TILES - 2 else nc.vector.tensor_copy
            for half in halves:
                copy(
                    out=words[:, 2 * half : 2 * half + 2, :, :],
                    in_=turned_of[(i, half)][:].rearrange("p g u q -> p g q u"),
                )

        def quantise_and_multiply(i, halves=(0, 1)):
            if halves[0] == 0:
                codes_of[i] = tail.tile(
                    [P, PASSES * P], U32, name="codes", tag="codes", align_bytes=64
                )
                scales_of[i] = tail.tile(
                    [P, PASSES * P], U8, name="scales", tag="scales", align_bytes=64
                )
                product_of[i] = psum_out.tile([P, DV], F32, name="product", tag="product")
            codes, scales = codes_of[i], scales_of[i]
            passes = range(halves[0] * PASSES // 2, (halves[-1] + 1) * PASSES // 2)
            words = slice(passes[0] * P, (passes[-1] + 1) * P)
            nc.vector.quantize_mx(
                out=codes[:, words].bitcast(FP8X4), scales=scales[:, words],
                in_=grouped_of[i][:, passes[0] * P * PACK : (passes[-1] + 1) * P * PACK],
            )
            for g in passes:
                nc.tensor.matmul_mx(
                    out=product_of[i][:],
                    lhsT=codes[:, g * P : (g + 1) * P].bitcast(FP8X4),
                    lhsT_scale=scales[:, g * P : (g + 1) * P],
                    rhs=v_codes[:, g * DV : (g + 1) * DV].bitcast(FP8X4),
                    rhs_scale=v_scales[:, g * DV : (g + 1) * DV],
                    start=(g == 0),
                    stop=(g == PASSES - 1),
                )

        def store(i):
            result = tail.tile([P, DV], F32, name="result", tag="result", bufs=4)
            nc.vector.tensor_copy(out=result[:], in_=product_of[i][:])
            nc.sync.dma_start(out=out[i * P : (i + 1) * P, :], in_=result[:])

        groups = []
        for size in GROUP_SIZES:
            first = sum(len(group) for group in groups)
            groups.append(list(range(first, first + size)))

        def tiles_of(g):
            return groups[g] if 0 <= g < len(groups) else []

        def distance_terms(i):
            t0 = i + CHUNK - 1
            preparing = i % CHUNK == 1 and t0 < Q_TILES
            if preparing:
                take = turn_queries(t0)
            scaled_differences(i)
            if preparing:
                take()

        def finish_minima(group):
            cols = slice(group[0], group[-1] + 1)
            nc.vector.tensor_add(
                out=h_pair[:, 1, cols], in0=h_pair[:, 0, cols], in1=a_q[:, cols]
            )

        def minimum_terms(group):
            cols = slice(group[0], group[-1] + 1)
            nc.vector.tensor_add(
                out=inv_s_min[:, cols], in0=r_pair[:, 0, cols], in1=r_pair[:, 1, cols]
            )
            nc.vector.reciprocal(out=inv_s_min[:, cols], in_=inv_s_min[:, cols])
            nc.vector.tensor_mul(
                out=shift[:, cols], in0=inv_s_min[:, cols], in1=inv_s_min[:, cols]
            )
            nc.vector.tensor_scalar(
                out=inv_s_min_sq[:, cols], in0=shift[:, cols], scalar1=2.0, scalar2=None,
                op0=ALU.mult,
            )
            nc.vector.tensor_mul(out=shift[:, cols], in0=shift[:, cols], in1=a_q[:, cols])

        def logarithm(i):
            col = slice(i, i + 1)
            if has_one_root(i):
                nc.scalar.activation(
                    out=row_of[i][:], in_=row_of[i][:], func=ACT.Ln,
                    scale=inv_s_min_sq[:, col], bias=shift[:, col],
                )
            else:
                nc.scalar.activation(
                    out=row_of[i][:], in_=row_of[i][:], func=ACT.Ln, scale=inv_s_min[:, col]
                )

        def exponential(i):
            power = neg_half_p if has_one_root(i) else neg_p
            nc.scalar.activation(
                out=row_of[i][:], in_=row_of[i][:], func=ACT.Exp, scale=power[:, 0:1],
                accum_out=e_sum[:, i : i + 1],
            )

        for banks in BANK_HALVES:
            for bank in banks:
                spread(kb_neg_row, kb_neg, bank * TURNS, psum_turn, "turn", nc.scalar.copy)
            scores(0, banks)
        query_norms(CHUNK)
        query_norms(2 * CHUNK)
        for t0 in (0, CHUNK):
            turn_norms(k_feats, t0, psum_turn, "turn", nc.scalar.copy, kT_norm)
        turn_norms(q_feats, 0, psum_turn, "turn", nc.scalar.copy, qT_norm)

        v_grouped = rows.tile([P, PASSES, DV, PACK], BF16, name="v_grouped", tag="row", align_bytes=64)
        for g in range(PASSES):
            nc.gpsimd.tensor_scalar(
                out=v_grouped[:, g, :, :], in0=v_raw[:, g, :, :].rearrange("p j w -> p w j"),
                scalar1=1.0, scalar2=0.0, op0=ALU.mult, op1=ALU.add,
            )

        def later_terms(tiles):
            half_norms(nc.gpsimd, tiles)
            query_terms(nc.gpsimd, tiles)
            split_norms(q_feats, 3, uu, tiles)

        later_terms(slice(CHUNK, 3 * CHUNK))

        def root_minima(group):
            cols = slice(group[0], group[-1] + 1)
            nc.scalar.activation(out=r_pair[:, :, cols], in_=h_pair[:, :, cols], func=ACT.Sqrt)

        def add_roots(i):
            for piece in range(0 if adds_on_vector(i) else ADD_PIECES):
                part = slice(piece * NK // ADD_PIECES, (piece + 1) * NK // ADD_PIECES)
                nc.gpsimd.tensor_add(
                    out=row_of[i][:, part], in0=row_of[i][:, part], in1=root_of[i][:, part]
                )

        for i in groups[0]:
            distance_terms(i)
            floor_and_min(i)
            if i == groups[0][-1]:
                finish_minima(groups[0])
                root_minima(groups[0])
            square_roots(i)
            if i == 0:
                query_norms(3 * CHUNK)
            add_roots(i)
            if i == 0:
                later_terms(slice(3 * CHUNK, Q_TILES))

        nc.vector.reciprocal(out=neg_p[:], in_=neg_p[:])
        nc.vector.tensor_scalar(
            out=neg_p[:], in0=neg_p[:], scalar1=-2.0, scalar2=None, op0=ALU.mult
        )
        neg_half_p = keep.tile([P, 1], F32, name="neg_half_p")
        nc.vector.tensor_scalar(
            out=neg_half_p[:], in0=neg_p[:], scalar1=0.5, scalar2=None, op0=ALU.mult
        )
        v_codes = keep.tile([P, PASSES * DV], U32, name="v_codes", align_bytes=64)
        v_scales = keep.tile([P, PASSES * DV], U8, name="v_scales", align_bytes=64)
        nc.vector.quantize_mx(
            out=v_codes[:].bitcast(FP8X4),
            scales=v_scales[:],
            in_=v_grouped[:].rearrange("p g w j -> p (g w j)"),
        )

        for g in range(len(groups) + 1):
            cur, old, nxt = tiles_of(g), tiles_of(g - 1), tiles_of(g + 1)
            if g == 0:
                minimum_terms(cur)
            if cur and g > 0:
                root_minima(cur)
                for i in cur:
                    if has_one_root(i) and i not in root_of:
                        product_under_root(i)
                    square_roots(i)
                    add_roots(i)

            if g > 0 and cur and not nxt:
                minimum_terms(cur)
            weighed = list(cur[:4] if g == 0 else cur[:3]) if nxt else []
            points = 2 * len(nxt) - len(weighed)

            def point(k):
                if weighed and k >= points:
                    normalise(weighed.pop(0))

            if old:
                if old[0] not in weights_of:
                    normalise(old[0])
                turn_weights(old[0])
            for j in range(max(len(old) + 1, len(nxt), 1)):
                if j < len(nxt):
                    distance_terms(nxt[j])
                point(2 * j)
                split = not cur and j == len(old) - 2
                if j + 1 < len(old) and old[j + 1] not in weights_of:
                    normalise(old[j + 1], (0,) if split else (0, 1))
                    if split:
                        normalise(old[j + 1], (1,))
                if j < len(old):
                    group_weights(old[j])
                if j + 1 < len(old):
                    turn_weights(old[j + 1])
                if j < len(nxt):
                    floor_and_min(nxt[j])
                    if has_one_root(nxt[j]) and product_on_gpsimd(nxt[j]):
                        product_under_root(nxt[j])
                if j == 0 and cur:
                    if g > 0 and nxt:
                        minimum_terms(cur)
                    for i in cur:
                        if not adds_on_vector(i):
                            logarithm(i)
                for i in cur:
                    if adds_on_vector(i) and j == max(1, i - 13):
                        nc.vector.tensor_add(
                            out=row_of[i][:], in0=row_of[i][:], in1=root_of[i][:]
                        )
                        logarithm(i)
                if cur and j == (max([max(1, i - 13) for i in cur if adds_on_vector(i)], default=0)):
                    for i in cur:
                        exponential(i)
                if j < len(old) and not cur and j == len(old) - 1:
                    quantise_and_multiply(old[j], (0,))
                    quantise_and_multiply(old[j], (1,))
                elif j < len(old):
                    quantise_and_multiply(old[j])
                if 0 <= j - 1 < len(old):
                    store(old[j - 1])
                point(2 * j + 1)
            if nxt:
                finish_minima(nxt)
